import numpy as np
import ml_dtypes


def mxq(x, axis, fmt="e4m3"):
    dtype, down = {"e4m3": (ml_dtypes.float8_e4m3fn, 7), "e5m2": (ml_dtypes.float8_e5m2, 14)}[fmt]
    v = np.moveaxis(np.asarray(x, np.float32).astype(ml_dtypes.bfloat16).astype(np.float64), axis, -1)
    blocks = v.reshape(v.shape[:-1] + (-1, 32))
    amax = np.abs(blocks).max(-1, keepdims=True)
    byte = np.maximum(np.where(amax > 0, np.frexp(amax)[1] - 1 + 127, 0) - down, 1)
    scale = np.exp2(byte - 127.0)
    codes = (blocks / scale).astype(np.float32).astype(dtype).astype(np.float64)
    return np.moveaxis((codes * scale).reshape(v.shape), -1, axis)


WIDE = False


def mx_kscale(k):
    if not WIDE:
        return np.ones(k)
    levels = np.array([10, -10, 5, -5, 0])
    if k % 512:
        return np.exp2(np.random.permutation(np.resize(levels, k // 32))).repeat(32)
    a = np.empty((k // 512, 16))
    for p in range(k // 512):
        a[p, :8] = np.random.permutation(np.resize(levels, 8))
        for g in range(8):
            far = levels[np.abs(levels - a[p, g]) >= 10]
            a[p, g + 8] = far[np.random.randint(len(far))]
    return np.exp2(a.ravel()).repeat(32)


BF16 = ml_dtypes.bfloat16


def bf(x):
    return np.asarray(x, np.float32).astype(BF16)


def f64(x):
    return np.asarray(x).astype(np.float64)


B, HI, WI, F, D, NH, C = 1, 32, 32, 1024, 256, 3, 16
N = HI * WI
EPS = 1e-12


def l2norm_rows(a):
    n = np.sqrt(np.sum(a * a, axis=1, keepdims=True))
    return a / np.maximum(n, EPS)


def draw0():
    s = mx_kscale(F)

    def w():
        return bf(np.random.standard_normal((D, F)) / np.sqrt(F) / s[None, :])

    def b():
        return bf(np.random.standard_normal(D) * 0.2)

    return {"x": bf(np.random.standard_normal((B, F, HI, WI)) * s[None, :, None, None]),
            "W1": w(), "b1": b(), "W2": w(), "b2": b(), "W3": w(), "b3": b()}


def core(x, W1, b1, W2, b2, W3, b3):
    xq = mxq(f64(x).reshape(F, N).T, 1, "e4m3")
    heads = [l2norm_rows((xq @ mxq(f64(W), 1, "e4m3").T) + f64(b)) for W, b in ((W1, b1), (W2, b2), (W3, b3))]
    return np.stack(heads)


def e4m3fn_bytes(y):
    return np.clip(np.asarray(y, np.float64), -448.0, 448.0).astype(np.float32).astype(ml_dtypes.float8_e4m3fn).view(np.uint8)


def e4m3fn_values(b):
    return np.asarray(b, np.uint8).view(ml_dtypes.float8_e4m3fn).astype(np.float64)


def setup_inputs():
    d = draw0()
    x0 = np.asarray(d['x']).astype(np.float64)
    s = (np.max(np.abs(x0), axis=(0, 2, 3), keepdims=True) / 448.0).astype(np.float32)
    out = {}
    for k, v in d.items():
        if k == 'x':
            out['x_bytes'] = e4m3fn_bytes(x0 / s.astype(np.float64))
            out['x_scale'] = s
        else:
            out[k] = v
    return out


def reference(x_bytes, x_scale, W1, b1, W2, b2, W3, b3):
    return core(e4m3fn_values(x_bytes) * x_scale.astype(np.float64), W1, b1, W2, b2, W3, b3)

@@ -1,0 +1,229 @@
+from contextlib import ExitStack
+
+import concourse.mybir as mybir
+from concourse.masks import make_identity
+
+F32 = mybir.dt.float32
+BF16 = mybir.dt.bfloat16
+U32 = mybir.dt.uint32
+U8 = mybir.dt.uint8
+FP8 = mybir.dt.float8_e4m3fn
+FP8X4 = mybir.dt.float8_e4m3fn_x4
+ACT = mybir.ActivationFunctionType
+ALU = mybir.AluOpType
+
+P = 128
+NODES = 1024
+FEAT = 1024
+D = 256
+HEADS = 3
+G = 2
+CH = 256
+NCH = NODES // CH
+FLOPS = 2 * NODES * FEAT * D * HEADS
+
+NWARM = 4
+V_WIDEN = ((1, 0, 0), (1, 0, 1), (1, 0, 2), (1, 0, 3), (0, 1, 2), (0, 1, 3))
+S_SCALE = ((1, 1, 2), (2, 1, 1), (2, 1, 2), (3, 0, 2), (3, 1, 0), (3, 1, 1), (3, 1, 2))
+
+
+def tile_gat_pa_kernel(tc, x_bytes, x_scale, W1, b1, W2, b2, W3, b3, out):
+    nc = tc.nc
+    Ws = (W1, W2, W3)
+    with ExitStack() as ctx:
+        keep = ctx.enter_context(tc.tile_pool(name="keep", bufs=1))
+        psum = ctx.enter_context(tc.psum_pool(name="psum", bufs=1))
+        ctx.enter_context(tc.manual_schedule())
+
+        def bank(k, name):
+            return psum.tile([P, 512], F32, name=name, tag="bank%d" % (k % 8))
+
+        one1 = keep.tile([P, 1], F32, name="one1")
+        nc.vector.memset(one1[:], 1.0)
+        ones = keep.tile([P, P], BF16, name="ones")
+        nc.vector.memset(ones[:], 1.0)
+        ident = keep.tile([P, P], F32, name="ident")
+        make_identity(nc, ident[:])
+
+        warm = keep.tile([P, 1], F32, name="warm")
+        nc.scalar.activation(out=warm[:], in_=one1[:], func=ACT.Sqrt)
+        xv = x_bytes[0].rearrange("(g p t) h w -> p g t (h w)", g=G, p=P, t=4)
+        xs = keep.tile([P, G, 4], F32, name="xs")
+        nc.sync.dma_start(out=xs[:], in_=x_scale[0].rearrange("(g p t) a b -> p g (t a b)", g=G, p=P, t=4))
+        xb = []
+        for g in range(G):
+            xbg = keep.tile([P, 4, NODES], U8, name="xb%d" % g)
+            nc.sync.dma_start(out=xbg[:], in_=xv[:, g, :, :])
+            xb.append(xbg)
+        wraw = []
+        for h in range(HEADS):
+            wr = keep.tile([P, 2, FEAT], BF16, name="wraw%d" % h)
+            nc.sync.dma_start(out=wr[:], in_=Ws[h].rearrange("(a p) k -> p a k", p=P))
+            wraw.append(wr)
+        bias = keep.tile([P, 4 * D], BF16, name="bias")
+        for i, b in enumerate((b1, b2, b3)):
+            nc.sync.dma_start(out=bias[:, i * D:(i + 1) * D], in_=b.partition_broadcast(P))
+        nc.gpsimd.tensor_copy(out=bias[:, 3 * D:4 * D], in_=bias[:, 2 * D:3 * D])
+
+        wq = keep.tile([P, G, HEADS * D], U32, name="wq", align_bytes=64)
+        wsc = keep.tile([P, G, HEADS * D], U8, name="wsc", align_bytes=64)
+        junk = keep.tile([P, D], BF16, name="junk")
+        outv = out.rearrange("h (q p) d -> q p h d", p=P)
+        xw, xg, xq, xsc, hh, oo, ss, rr, rm, ri = [], [], [], [], [], [], [], [], [], []
+        for c in range(NCH):
+            xg.append(keep.tile([P, G, CH, 4], BF16, name="xg%d" % c, align_bytes=64))
+            xq.append(keep.tile([P, G, CH], U32, name="xq%d" % c, align_bytes=64))
+            xsc.append(keep.tile([P, G, CH], U8, name="xsc%d" % c, align_bytes=64))
+            hh.append(keep.tile([P, 2, HEADS * D], F32, name="hh%d" % c))
+            oo.append(keep.tile([P, 2, HEADS * D], F32, name="oo%d" % c))
+            ss.append(keep.tile([P, 2 * HEADS], F32, name="ss%d" % c))
+            rr.append(keep.tile([P, 2 * HEADS], F32, name="rr%d" % c))
+            rm.append(keep.tile([P, 2 * HEADS], F32, name="rm%d" % c))
+            ri.append(keep.tile([P, 2 * HEADS], F32, name="ri%d" % c))
+        xw.append(keep.tile([P, G, 4, CH], BF16, name="xw0"))
+        xw.append(keep.tile([P, G, 4, CH], BF16, name="xw1"))
+        xw23 = keep.tile([P, G, 4, 2 * CH], BF16, name="xw23")
+        wt, wg = {}, {}
+
+        def dummy(k):
+            dm = bank(k, "dm")
+            nc.tensor.matmul(out=dm[:], lhsT=ones[:], rhs=xw[0][:, 0, 0:2, :].rearrange("p t n -> p (t n)"), start=True, stop=True)
+
+        def widen(c, g, t):
+            src = xb[g][:, t, c * CH:(c + 1) * CH].bitcast(FP8)
+            if (c, g, t) in V_WIDEN:
+                nc.vector.tensor_scalar(out=xw[c][:, g, t, :], in0=src, scalar1=xs[:, g, t:t + 1], scalar2=None, op0=ALU.mult)
+            else:
+                nc.scalar.activation(out=xw[c][:, g, t, :], in_=src, func=ACT.Copy, scale=xs[:, g, t:t + 1])
+
+        def widen23(g, t):
+            nc.scalar.activation(out=xw23[:, g, t, :], in_=xb[g][:, t, 2 * CH:4 * CH].bitcast(FP8), func=ACT.Copy, scale=xs[:, g, t:t + 1])
+
+        def inter(c):
+            src = xw[c][:] if c < 2 else xw23[:, :, :, (c - 2) * CH:(c - 1) * CH]
+            nc.vector.tensor_copy(out=xg[c][:], in_=src.rearrange("p g t n -> p g n t"))
+
+        def xquant(c):
+            nc.vector.quantize_mx(out=xq[c][:].rearrange("p g n -> p (g n)").bitcast(FP8X4), scales=xsc[c][:].rearrange("p g n -> p (g n)"), in_=xg[c][:].rearrange("p g n t -> p (g n t)"))
+
+        def wtrans(h, g):
+            words = wraw[h][:].rearrange("p a k -> p (a k)").bitcast(F32)
+            w = bank(2 * h + g, "wt")
+            wt[(h, g)] = w
+            for a in range(2):
+                for u in range(2):
+                    base = a * 512 + g * 256
+                    nc.tensor.transpose(out=w[:, u * D + a * P:u * D + (a + 1) * P], in_=words[:, base + u:base + 256:2], identity=ident[:])
+
+        def wcopy(h, g, eng):
+            wg[(h, g)] = keep.tile([P, 4 * D], BF16, name="wg%d%d" % (h, g), align_bytes=64)
+            dst = wg[(h, g)][:].bitcast(F32).rearrange("p (c u) -> p c u", u=2)
+            src = wt[(h, g)][:].rearrange("p (u c) -> p c u", u=2)
+            if eng == "S":
+                nc.scalar.copy(out=dst, in_=src)
+            else:
+                nc.vector.tensor_copy(out=dst, in_=src)
+
+        def wquant(h, g):
+            nc.vector.quantize_mx(out=wq[:, g, h * D:(h + 1) * D].bitcast(FP8X4), scales=wsc[:, g, h * D:(h + 1) * D], in_=wg[(h, g)][:])
+
+        pa, pb = {}, {}
+
+        def mm(c):
+            pb[c] = bank(3 * c + 2, "pb")
+            for j in range(2):
+                pa[(c, j)] = bank(3 * c + j, "pa")
+                cols = slice(j * P, (j + 1) * P)
+                for g in range(G):
+                    nc.tensor.matmul_mx(out=pa[(c, j)][:], lhsT=xq[c][:, g, cols].bitcast(FP8X4), lhsT_scale=xsc[c][:, g, cols], rhs=wq[:, g, 0:512].bitcast(FP8X4), rhs_scale=wsc[:, g, 0:512], start=(g == 0), stop=(g == G - 1))
+                    nc.tensor.matmul_mx(out=pb[c][:, j * D:(j + 1) * D], lhsT=xq[c][:, g, cols].bitcast(FP8X4), lhsT_scale=xsc[c][:, g, cols], rhs=wq[:, g, 512:768].bitcast(FP8X4), rhs_scale=wsc[:, g, 512:768], start=(g == 0), stop=(g == G - 1))
+
+        def badd_a(c, j):
+            nc.vector.tensor_tensor(out=hh[c][:, j, 0:512], in0=pa[(c, j)][:], in1=bias[:, 0:512], op=ALU.add)
+
+        def badd_b(c):
+            nc.vector.tensor_tensor(out=hh[c][:, :, 512:768], in0=pb[c][:].rearrange("p (j d) -> p j d", j=2), in1=bias[:, 512:1024].rearrange("p (j d) -> p j d", j=2), op=ALU.add)
+
+        def square(c):
+            for h in (0, 1, 2):
+                for j in range(2):
+                    k = j * HEADS + h
+                    nc.scalar.activation(out=junk[:], in_=hh[c][:, j, h * D:(h + 1) * D], func=ACT.Square, accum_out=ss[c][:, k:k + 1])
+            nc.scalar.activation(out=rr[c][:], in_=ss[c][:], func=ACT.Sqrt)
+
+        def rmax(c):
+            nc.vector.tensor_scalar_max(out=rm[c][:], in0=rr[c][:], scalar1=1e-12)
+
+        def rcp(c):
+            nc.vector.reciprocal(out=ri[c][:], in_=rm[c][:])
+
+        def scale(c):
+            for j in range(2):
+                for h in range(HEADS):
+                    k = j * HEADS + h
+                    dst, src = oo[c][:, j, h * D:(h + 1) * D], hh[c][:, j, h * D:(h + 1) * D]
+                    if (c, j, h) in S_SCALE:
+                        nc.scalar.activation(out=dst, in_=src, func=ACT.Copy, scale=ri[c][:, k:k + 1])
+                    else:
+                        nc.vector.tensor_scalar(out=dst, in0=src, scalar1=ri[c][:, k:k + 1], scalar2=None, op0=ALU.mult)
+                nc.sync.dma_start(out=outv[2 * c + j], in_=oo[c][:, j, :].rearrange("p (h d) -> p h d", h=HEADS))
+
+        for t in range(4):
+            widen(0, 0, t)
+        for i in range(NWARM):
+            dummy(i)
+        for t in range(4):
+            widen(1, 0, t)
+        for t in range(4):
+            widen(0, 1, t)
+        inter(0)
+        for t in range(4):
+            widen(1, 1, t)
+        wtrans(0, 0)
+        wtrans(0, 1)
+        for t in range(4):
+            widen23(0, t)
+        inter(1)
+        xquant(0)
+        wcopy(0, 0, "S")
+        wcopy(0, 1, "S")
+        wtrans(1, 0)
+        wtrans(1, 1)
+        wquant(0, 0)
+        xquant(1)
+        wquant(0, 1)
+        for t in range(4):
+            widen23(1, t)
+        inter(2)
+        wcopy(1, 0, "S")
+        wcopy(1, 1, "S")
+        wtrans(2, 0)
+        wtrans(2, 1)
+        wquant(1, 0)
+        wquant(1, 1)
+        xquant(2)
+        wcopy(2, 0, "S")
+        wcopy(2, 1, "S")
+        wquant(2, 0)
+        wquant(2, 1)
+        mm(0)
+        mm(1)
+        inter(3)
+        badd_a(0, 0)
+        xquant(3)
+        badd_a(0, 1)
+        badd_b(0)
+        square(0)
+        for c in range(1, NCH):
+            badd_a(c, 0)
+            badd_a(c, 1)
+            rmax(c - 1)
+            badd_b(c)
+            rcp(c - 1)
+            if c + 1 < NCH:
+                mm(c + 1)
+            square(c)
+            scale(c - 1)
+        rmax(NCH - 1)
+        rcp(NCH - 1)
+        scale(NCH - 1)

@@ -19,12 +19,13 @@ D = 256
 HEADS = 3
 G = 2
 CH = 256
-NCH = NODES // CH
 FLOPS = 2 * NODES * FEAT * D * HEADS
 
-NWARM = 4
-V_WIDEN = ((1, 0, 0), (1, 0, 1), (1, 0, 2), (1, 0, 3), (0, 1, 2), (0, 1, 3))
-S_SCALE = ((1, 1, 2), (2, 1, 1), (2, 1, 2), (3, 0, 2), (3, 1, 0), (3, 1, 1), (3, 1, 2))
+N_WARM_F32 = 8
+N_WARM_BF16 = 3
+N_V_SCALE = 3
+BATCHES = tuple((pair, h) for pair in range(2) for h in range(HEADS))
+UNIT_BANK = (7, 6, 0, 1, 2, 3, 4, 5, 7, 6, 0, 1)
 
 
 def tile_gat_pa_kernel(tc, x_bytes, x_scale, W1, b1, W2, b2, W3, b3, out):
@@ -35,195 +36,202 @@ def tile_gat_pa_kernel(tc, x_bytes, x_scale, W1, b1, W2, b2, W3, b3, out):
         psum = ctx.enter_context(tc.psum_pool(name="psum", bufs=1))
         ctx.enter_context(tc.manual_schedule())
 
-        def bank(k, name):
-            return psum.tile([P, 512], F32, name=name, tag="bank%d" % (k % 8))
+        def bank(k, name, shape, dtype):
+            return psum.tile(shape, dtype, name=name, tag="bank%d" % k)
 
         one1 = keep.tile([P, 1], F32, name="one1")
         nc.vector.memset(one1[:], 1.0)
+        brow = keep.tile([P, HEADS * D], BF16, name="brow")
+        nc.vector.memset(brow[:], 0.0)
         ones = keep.tile([P, P], BF16, name="ones")
         nc.vector.memset(ones[:], 1.0)
         ident = keep.tile([P, P], F32, name="ident")
         make_identity(nc, ident[:])
 
+        xs = keep.tile([P, G, 4], F32, name="xs")
+        nc.scalar.dma_start(out=xs[:], in_=x_scale[0].rearrange("(g p t) a b -> p g (t a b)", g=G, p=P, t=4))
+        for i, b in enumerate((b1, b2, b3)):
+            nc.scalar.dma_start(out=brow[0:1, i * D:(i + 1) * D], in_=b.rearrange("(o d) -> o d", o=1))
         warm = keep.tile([P, 1], F32, name="warm")
         nc.scalar.activation(out=warm[:], in_=one1[:], func=ACT.Sqrt)
         xv = x_bytes[0].rearrange("(g p t) h w -> p g t (h w)", g=G, p=P, t=4)
-        xs = keep.tile([P, G, 4], F32, name="xs")
-        nc.sync.dma_start(out=xs[:], in_=x_scale[0].rearrange("(g p t) a b -> p g (t a b)", g=G, p=P, t=4))
-        xb = []
+        xb = {}
         for g in range(G):
-            xbg = keep.tile([P, 4, NODES], U8, name="xb%d" % g)
-            nc.sync.dma_start(out=xbg[:], in_=xv[:, g, :, :])
-            xb.append(xbg)
+            for t in range(4):
+                xb[(g, t)] = keep.tile([P, NODES], U8, name="xb%d%d" % (g, t))
+                nc.sync.dma_start(out=xb[(g, t)][:], in_=xv[:, g, t, :])
         wraw = []
         for h in range(HEADS):
             wr = keep.tile([P, 2, FEAT], BF16, name="wraw%d" % h)
             nc.sync.dma_start(out=wr[:], in_=Ws[h].rearrange("(a p) k -> p a k", p=P))
             wraw.append(wr)
-        bias = keep.tile([P, 4 * D], BF16, name="bias")
-        for i, b in enumerate((b1, b2, b3)):
-            nc.sync.dma_start(out=bias[:, i * D:(i + 1) * D], in_=b.partition_broadcast(P))
-        nc.gpsimd.tensor_copy(out=bias[:, 3 * D:4 * D], in_=bias[:, 2 * D:3 * D])
 
+        bias = keep.tile([P, HEADS * D], BF16, name="bias")
         wq = keep.tile([P, G, HEADS * D], U32, name="wq", align_bytes=64)
         wsc = keep.tile([P, G, HEADS * D], U8, name="wsc", align_bytes=64)
         junk = keep.tile([P, D], BF16, name="junk")
-        outv = out.rearrange("h (q p) d -> q p h d", p=P)
-        xw, xg, xq, xsc, hh, oo, ss, rr, rm, ri = [], [], [], [], [], [], [], [], [], []
-        for c in range(NCH):
+        xw = [keep.tile([P, G, 4, 2 * CH], BF16, name="xw%d" % pair) for pair in range(2)]
+        xg, xq, xsc, hh, oo = [], [], [], [], []
+        for c in range(4):
             xg.append(keep.tile([P, G, CH, 4], BF16, name="xg%d" % c, align_bytes=64))
             xq.append(keep.tile([P, G, CH], U32, name="xq%d" % c, align_bytes=64))
             xsc.append(keep.tile([P, G, CH], U8, name="xsc%d" % c, align_bytes=64))
-            hh.append(keep.tile([P, 2, HEADS * D], F32, name="hh%d" % c))
-            oo.append(keep.tile([P, 2, HEADS * D], F32, name="oo%d" % c))
-            ss.append(keep.tile([P, 2 * HEADS], F32, name="ss%d" % c))
-            rr.append(keep.tile([P, 2 * HEADS], F32, name="rr%d" % c))
-            rm.append(keep.tile([P, 2 * HEADS], F32, name="rm%d" % c))
-            ri.append(keep.tile([P, 2 * HEADS], F32, name="ri%d" % c))
-        xw.append(keep.tile([P, G, 4, CH], BF16, name="xw0"))
-        xw.append(keep.tile([P, G, 4, CH], BF16, name="xw1"))
-        xw23 = keep.tile([P, G, 4, 2 * CH], BF16, name="xw23")
-        wt, wg = {}, {}
+            hh.append(keep.tile([P, 2, HEADS, D], F32, name="hh%d" % c))
+            oo.append(keep.tile([P, 2, HEADS, D], F32, name="oo%d" % c))
+        ss, rr, rm, ri = {}, {}, {}, {}
+        for b in BATCHES:
+            ss[b] = keep.tile([P, 4], F32, name="ss%d%d" % b)
+            rr[b] = keep.tile([P, 4], F32, name="rr%d%d" % b)
+            rm[b] = keep.tile([P, 4], F32, name="rm%d%d" % b)
+            ri[b] = keep.tile([P, 4], F32, name="ri%d%d" % b)
+        wt, wg, pu = {}, {}, {}
+        outv = out.rearrange("h (q p) d -> h q p d", p=P)
 
-        def dummy(k):
-            dm = bank(k, "dm")
-            nc.tensor.matmul(out=dm[:], lhsT=ones[:], rhs=xw[0][:, 0, 0:2, :].rearrange("p t n -> p (t n)"), start=True, stop=True)
+        def warm_f32():
+            dm = bank(7, "dmf", [P, P], F32)
+            nc.tensor.matmul(out=dm[:], lhsT=ident[:], rhs=ident[:], start=True, stop=True)
 
-        def widen(c, g, t):
-            src = xb[g][:, t, c * CH:(c + 1) * CH].bitcast(FP8)
-            if (c, g, t) in V_WIDEN:
-                nc.vector.tensor_scalar(out=xw[c][:, g, t, :], in0=src, scalar1=xs[:, g, t:t + 1], scalar2=None, op0=ALU.mult)
+        def warm_bf16():
+            dm = bank(7, "dmb", [P, 512], F32)
+            nc.tensor.matmul(out=dm[:], lhsT=ones[:], rhs=xw[0][:, 1, 0, :], start=True, stop=True)
+
+        def bias_matmul():
+            bp = bank(6, "bp", [P, 1024], BF16)
+            pu["bias"] = bp
+            nc.tensor.matmul(out=bp[:, 0:512], lhsT=ones[:], rhs=brow[:, 0:512], start=True, stop=True)
+            nc.tensor.matmul(out=bp[:, 512:768], lhsT=ones[:], rhs=brow[:, 512:768], start=True, stop=True)
+
+        def bias_copy():
+            nc.scalar.copy(out=bias[:], in_=pu["bias"][:, 0:768])
+
+        def widen(pair, g, t):
+            src = xb[(g, t)][:, pair * 512:(pair + 1) * 512].bitcast(FP8)
+            if pair == 0:
+                nc.vector.tensor_scalar(out=xw[pair][:, g, t, :], in0=src, scalar1=xs[:, g, t:t + 1], scalar2=None, op0=ALU.mult)
             else:
-                nc.scalar.activation(out=xw[c][:, g, t, :], in_=src, func=ACT.Copy, scale=xs[:, g, t:t + 1])
+                nc.scalar.activation(out=xw[pair][:, g, t, :], in_=src, func=ACT.Copy, scale=xs[:, g, t:t + 1])
 
-        def widen23(g, t):
-            nc.scalar.activation(out=xw23[:, g, t, :], in_=xb[g][:, t, 2 * CH:4 * CH].bitcast(FP8), func=ACT.Copy, scale=xs[:, g, t:t + 1])
-
-        def inter(c):
-            src = xw[c][:] if c < 2 else xw23[:, :, :, (c - 2) * CH:(c - 1) * CH]
-            nc.vector.tensor_copy(out=xg[c][:], in_=src.rearrange("p g t n -> p g n t"))
+        def inter(c, eng):
+            src = xw[c // 2][:, :, :, (c % 2) * CH:(c % 2 + 1) * CH].rearrange("p g t n -> p g n t")
+            if eng == "S":
+                nc.scalar.copy(out=xg[c][:], in_=src)
+            else:
+                nc.vector.tensor_copy(out=xg[c][:], in_=src)
 
         def xquant(c):
             nc.vector.quantize_mx(out=xq[c][:].rearrange("p g n -> p (g n)").bitcast(FP8X4), scales=xsc[c][:].rearrange("p g n -> p (g n)"), in_=xg[c][:].rearrange("p g n t -> p (g n t)"))
 
         def wtrans(h, g):
             words = wraw[h][:].rearrange("p a k -> p (a k)").bitcast(F32)
-            w = bank(2 * h + g, "wt")
+            w = bank(2 * h + g, "wt", [P, 512], F32)
             wt[(h, g)] = w
             for a in range(2):
                 for u in range(2):
                     base = a * 512 + g * 256
                     nc.tensor.transpose(out=w[:, u * D + a * P:u * D + (a + 1) * P], in_=words[:, base + u:base + 256:2], identity=ident[:])
 
-        def wcopy(h, g, eng):
+        def wcopy(h, g):
             wg[(h, g)] = keep.tile([P, 4 * D], BF16, name="wg%d%d" % (h, g), align_bytes=64)
-            dst = wg[(h, g)][:].bitcast(F32).rearrange("p (c u) -> p c u", u=2)
-            src = wt[(h, g)][:].rearrange("p (u c) -> p c u", u=2)
-            if eng == "S":
-                nc.scalar.copy(out=dst, in_=src)
-            else:
-                nc.vector.tensor_copy(out=dst, in_=src)
+            nc.scalar.copy(out=wg[(h, g)][:].bitcast(F32).rearrange("p (c u) -> p c u", u=2), in_=wt[(h, g)][:].rearrange("p (u c) -> p c u", u=2))
 
         def wquant(h, g):
             nc.vector.quantize_mx(out=wq[:, g, h * D:(h + 1) * D].bitcast(FP8X4), scales=wsc[:, g, h * D:(h + 1) * D], in_=wg[(h, g)][:])
 
-        pa, pb = {}, {}
+        def units(b):
+            return ((2 * b[0], b[1]), (2 * b[0] + 1, b[1]))
 
-        def mm(c):
-            pb[c] = bank(3 * c + 2, "pb")
-            for j in range(2):
-                pa[(c, j)] = bank(3 * c + j, "pa")
-                cols = slice(j * P, (j + 1) * P)
-                for g in range(G):
-                    nc.tensor.matmul_mx(out=pa[(c, j)][:], lhsT=xq[c][:, g, cols].bitcast(FP8X4), lhsT_scale=xsc[c][:, g, cols], rhs=wq[:, g, 0:512].bitcast(FP8X4), rhs_scale=wsc[:, g, 0:512], start=(g == 0), stop=(g == G - 1))
-                    nc.tensor.matmul_mx(out=pb[c][:, j * D:(j + 1) * D], lhsT=xq[c][:, g, cols].bitcast(FP8X4), lhsT_scale=xsc[c][:, g, cols], rhs=wq[:, g, 512:768].bitcast(FP8X4), rhs_scale=wsc[:, g, 512:768], start=(g == 0), stop=(g == G - 1))
-
-        def badd_a(c, j):
-            nc.vector.tensor_tensor(out=hh[c][:, j, 0:512], in0=pa[(c, j)][:], in1=bias[:, 0:512], op=ALU.add)
-
-        def badd_b(c):
-            nc.vector.tensor_tensor(out=hh[c][:, :, 512:768], in0=pb[c][:].rearrange("p (j d) -> p j d", j=2), in1=bias[:, 512:1024].rearrange("p (j d) -> p j d", j=2), op=ALU.add)
-
-        def square(c):
-            for h in (0, 1, 2):
+        def mm(b):
+            for c, h in units(b):
+                k = BATCHES.index(b) * 2 + c % 2
+                acc = bank(UNIT_BANK[k], "pu", [P, 2, D], F32)
+                pu[(c, h)] = acc
                 for j in range(2):
-                    k = j * HEADS + h
-                    nc.scalar.activation(out=junk[:], in_=hh[c][:, j, h * D:(h + 1) * D], func=ACT.Square, accum_out=ss[c][:, k:k + 1])
-            nc.scalar.activation(out=rr[c][:], in_=ss[c][:], func=ACT.Sqrt)
+                    cols = slice(j * P, (j + 1) * P)
+                    for g in range(G):
+                        nc.tensor.matmul_mx(out=acc[:, j, :], lhsT=xq[c][:, g, cols].bitcast(FP8X4), lhsT_scale=xsc[c][:, g, cols], rhs=wq[:, g, h * D:(h + 1) * D].bitcast(FP8X4), rhs_scale=wsc[:, g, h * D:(h + 1) * D], start=(g == 0), stop=(g == G - 1))
 
-        def rmax(c):
-            nc.vector.tensor_scalar_max(out=rm[c][:], in0=rr[c][:], scalar1=1e-12)
+        def badd(b, i):
+            c, h = units(b)[i]
+            nc.vector.tensor_tensor(out=hh[c][:, :, h, :], in0=pu[(c, h)][:], in1=bias[:, h * D:(h + 1) * D].unsqueeze(1).to_broadcast([P, 2, D]), op=ALU.add)
 
-        def rcp(c):
-            nc.vector.reciprocal(out=ri[c][:], in_=rm[c][:])
+        def square(b):
+            for i, (c, h) in enumerate(units(b)):
+                for j in range(2):
+                    nc.scalar.activation(out=junk[:], in_=hh[c][:, j, h, :], func=ACT.Square, accum_out=ss[b][:, 2 * i + j:2 * i + j + 1])
+            nc.scalar.activation(out=rr[b][:], in_=ss[b][:], func=ACT.Sqrt)
 
-        def scale(c):
-            for j in range(2):
-                for h in range(HEADS):
-                    k = j * HEADS + h
-                    dst, src = oo[c][:, j, h * D:(h + 1) * D], hh[c][:, j, h * D:(h + 1) * D]
-                    if (c, j, h) in S_SCALE:
-                        nc.scalar.activation(out=dst, in_=src, func=ACT.Copy, scale=ri[c][:, k:k + 1])
-                    else:
-                        nc.vector.tensor_scalar(out=dst, in0=src, scalar1=ri[c][:, k:k + 1], scalar2=None, op0=ALU.mult)
-                nc.sync.dma_start(out=outv[2 * c + j], in_=oo[c][:, j, :].rearrange("p (h d) -> p h d", h=HEADS))
+        def rmax(b):
+            nc.vector.tensor_scalar_max(out=rm[b][:], in0=rr[b][:], scalar1=1e-12)
 
-        for t in range(4):
-            widen(0, 0, t)
-        for i in range(NWARM):
-            dummy(i)
-        for t in range(4):
-            widen(1, 0, t)
-        for t in range(4):
-            widen(0, 1, t)
-        inter(0)
-        for t in range(4):
-            widen(1, 1, t)
-        wtrans(0, 0)
-        wtrans(0, 1)
-        for t in range(4):
-            widen23(0, t)
-        inter(1)
+        def rcp(b):
+            nc.vector.reciprocal(out=ri[b][:], in_=rm[b][:])
+
+        def scale(b, first, last, eng):
+            for k in range(first, last):
+                c, h = units(b)[k // 2]
+                j = k % 2
+                if eng == "S":
+                    nc.scalar.activation(out=oo[c][:, j, h, :], in_=hh[c][:, j, h, :], func=ACT.Copy, scale=ri[b][:, k:k + 1])
+                else:
+                    nc.vector.tensor_scalar(out=oo[c][:, j, h, :], in0=hh[c][:, j, h, :], scalar1=ri[b][:, k:k + 1], scalar2=None, op0=ALU.mult)
+                nc.sync.dma_start(out=outv[h, 2 * c + j], in_=oo[c][:, j, h, :])
+
+        for i in range(N_WARM_F32):
+            warm_f32()
+        bias_matmul()
+        for g in range(G):
+            for t in range(4):
+                widen(0, g, t)
+                widen(1, g, t)
+                if (g, t) == (1, 0):
+                    for i in range(N_WARM_BF16):
+                        warm_bf16()
+        bias_copy()
+        for h in range(2):
+            for g in range(G):
+                wtrans(h, g)
+        inter(0, "V")
+        inter(1, "V")
         xquant(0)
-        wcopy(0, 0, "S")
-        wcopy(0, 1, "S")
-        wtrans(1, 0)
-        wtrans(1, 1)
-        wquant(0, 0)
         xquant(1)
+        wcopy(0, 0)
+        wcopy(0, 1)
+        wquant(0, 0)
         wquant(0, 1)
-        for t in range(4):
-            widen23(1, t)
-        inter(2)
-        wcopy(1, 0, "S")
-        wcopy(1, 1, "S")
+        mm(BATCHES[0])
+        wcopy(1, 0)
+        wcopy(1, 1)
+        inter(2, "V")
+        inter(3, "S")
         wtrans(2, 0)
         wtrans(2, 1)
-        wquant(1, 0)
-        wquant(1, 1)
-        xquant(2)
-        wcopy(2, 0, "S")
-        wcopy(2, 1, "S")
-        wquant(2, 0)
-        wquant(2, 1)
-        mm(0)
-        mm(1)
-        inter(3)
-        badd_a(0, 0)
-        xquant(3)
-        badd_a(0, 1)
-        badd_b(0)
-        square(0)
-        for c in range(1, NCH):
-            badd_a(c, 0)
-            badd_a(c, 1)
-            rmax(c - 1)
-            badd_b(c)
-            rcp(c - 1)
-            if c + 1 < NCH:
-                mm(c + 1)
-            square(c)
-            scale(c - 1)
-        rmax(NCH - 1)
-        rcp(NCH - 1)
-        scale(NCH - 1)
+        for i, b in enumerate(BATCHES):
+            prev = BATCHES[i - 1] if i > 0 else None
+            badd(b, 0)
+            if prev:
+                rmax(prev)
+            badd(b, 1)
+            if prev:
+                rcp(prev)
+            if i < 2:
+                wquant(i + 1, 0)
+                wquant(i + 1, 1)
+            if i == 2:
+                xquant(3)
+            if i + 1 < len(BATCHES):
+                mm(BATCHES[i + 1])
+            if prev:
+                scale(prev, 0, N_V_SCALE, "V")
+            if i == 1:
+                xquant(2)
+            square(b)
+            if i == 0:
+                wcopy(2, 0)
+                wcopy(2, 1)
+            if prev:
+                scale(prev, N_V_SCALE, 4, "S")
+        last = BATCHES[-1]
+        rmax(last)
+        rcp(last)
+        scale(last, 0, 2, "V")
+        scale(last, 2, 4, "S")

@@ -21,11 +21,11 @@ G = 2
 CH = 256
 FLOPS = 2 * NODES * FEAT * D * HEADS
 
-N_WARM_F32 = 8
-N_WARM_BF16 = 3
 N_V_SCALE = 3
+N_DUMMY = 6
 BATCHES = tuple((pair, h) for pair in range(2) for h in range(HEADS))
-UNIT_BANK = (7, 6, 0, 1, 2, 3, 4, 5, 7, 6, 0, 1)
+UNIT_BANK = (6, 0, 1, 2, 3, 4, 5, 6, 0, 1, 2, 3)
+DUMMY_BANK = 7
 
 
 def tile_gat_pa_kernel(tc, x_bytes, x_scale, W1, b1, W2, b2, W3, b3, out):
@@ -69,7 +69,7 @@ def tile_gat_pa_kernel(tc, x_bytes, x_scale, W1, b1, W2, b2, W3, b3, out):
         bias = keep.tile([P, HEADS * D], BF16, name="bias")
         wq = keep.tile([P, G, HEADS * D], U32, name="wq", align_bytes=64)
         wsc = keep.tile([P, G, HEADS * D], U8, name="wsc", align_bytes=64)
-        junk = keep.tile([P, D], BF16, name="junk")
+        junk = keep.tile([P, len(BATCHES), 4, D], BF16, name="junk")
         xw = [keep.tile([P, G, 4, 2 * CH], BF16, name="xw%d" % pair) for pair in range(2)]
         xg, xq, xsc, hh, oo = [], [], [], [], []
         for c in range(4):
@@ -87,13 +87,9 @@ def tile_gat_pa_kernel(tc, x_bytes, x_scale, W1, b1, W2, b2, W3, b3, out):
         wt, wg, pu = {}, {}, {}
         outv = out.rearrange("h (q p) d -> h q p d", p=P)
 
-        def warm_f32():
-            dm = bank(7, "dmf", [P, P], F32)
-            nc.tensor.matmul(out=dm[:], lhsT=ident[:], rhs=ident[:], start=True, stop=True)
-
-        def warm_bf16():
-            dm = bank(7, "dmb", [P, 512], F32)
-            nc.tensor.matmul(out=dm[:], lhsT=ones[:], rhs=xw[0][:, 1, 0, :], start=True, stop=True)
+        def dummy():
+            dm = bank(DUMMY_BANK, "dm", [P, 512], F32)
+            nc.tensor.matmul(out=dm[:], lhsT=ones[:], rhs=xw[0][:, 0, 0, :], start=True, stop=True)
 
         def bias_matmul():
             bp = bank(6, "bp", [P, 1024], BF16)
@@ -157,7 +153,7 @@ def tile_gat_pa_kernel(tc, x_bytes, x_scale, W1, b1, W2, b2, W3, b3, out):
         def square(b):
             for i, (c, h) in enumerate(units(b)):
                 for j in range(2):
-                    nc.scalar.activation(out=junk[:], in_=hh[c][:, j, h, :], func=ACT.Square, accum_out=ss[b][:, 2 * i + j:2 * i + j + 1])
+                    nc.scalar.activation(out=junk[:, BATCHES.index(b), 2 * i + j, :], in_=hh[c][:, j, h, :], func=ACT.Square, accum_out=ss[b][:, 2 * i + j:2 * i + j + 1])
             nc.scalar.activation(out=rr[b][:], in_=ss[b][:], func=ACT.Sqrt)
 
         def rmax(b):
@@ -176,16 +172,14 @@ def tile_gat_pa_kernel(tc, x_bytes, x_scale, W1, b1, W2, b2, W3, b3, out):
                     nc.vector.tensor_scalar(out=oo[c][:, j, h, :], in0=hh[c][:, j, h, :], scalar1=ri[b][:, k:k + 1], scalar2=None, op0=ALU.mult)
                 nc.sync.dma_start(out=outv[h, 2 * c + j], in_=oo[c][:, j, h, :])
 
-        for i in range(N_WARM_F32):
-            warm_f32()
-        bias_matmul()
         for g in range(G):
             for t in range(4):
                 widen(0, g, t)
                 widen(1, g, t)
-                if (g, t) == (1, 0):
-                    for i in range(N_WARM_BF16):
-                        warm_bf16()
+                if (g, t) == (0, 0):
+                    for i in range(N_DUMMY):
+                        dummy()
+        bias_matmul()
         bias_copy()
         for h in range(2):
             for g in range(G):
@@ -205,6 +199,12 @@ def tile_gat_pa_kernel(tc, x_bytes, x_scale, W1, b1, W2, b2, W3, b3, out):
         inter(3, "S")
         wtrans(2, 0)
         wtrans(2, 1)
+        wquant(1, 0)
+        wquant(1, 1)
+        mm(BATCHES[1])
+        xquant(2)
+        wcopy(2, 0)
+        wcopy(2, 1)
         for i, b in enumerate(BATCHES):
             prev = BATCHES[i - 1] if i > 0 else None
             badd(b, 0)
@@ -213,21 +213,17 @@ def tile_gat_pa_kernel(tc, x_bytes, x_scale, W1, b1, W2, b2, W3, b3, out):
             badd(b, 1)
             if prev:
                 rcp(prev)
-            if i < 2:
-                wquant(i + 1, 0)
-                wquant(i + 1, 1)
-            if i == 2:
+            if i == 1:
+                wquant(2, 0)
+                wquant(2, 1)
+                mm(BATCHES[2])
                 xquant(3)
-            if i + 1 < len(BATCHES):
-                mm(BATCHES[i + 1])
+                mm(BATCHES[3])
+            if i >= 2 and i + 2 < len(BATCHES):
+                mm(BATCHES[i + 2])
             if prev:
                 scale(prev, 0, N_V_SCALE, "V")
-            if i == 1:
-                xquant(2)
             square(b)
-            if i == 0:
-                wcopy(2, 0)
-                wcopy(2, 1)
             if prev:
                 scale(prev, N_V_SCALE, 4, "S")
         last = BATCHES[-1]

@@ -153,7 +153,12 @@ def tile_gat_pa_kernel(tc, x_bytes, x_scale, W1, b1, W2, b2, W3, b3, out):
         def square(b):
             for i, (c, h) in enumerate(units(b)):
                 for j in range(2):
+                    if b == BATCHES[-1] and (i, j) == (1, 1):
+                        nc.vector.scalar_tensor_tensor(out=junk[:, BATCHES.index(b), 3, :], in0=hh[c][:, j, h, :], scalar=1.0, in1=hh[c][:, j, h, :], op0=ALU.mult, op1=ALU.mult, accum_out=ss[b][:, 3:4])
+                        continue
                     nc.scalar.activation(out=junk[:, BATCHES.index(b), 2 * i + j, :], in_=hh[c][:, j, h, :], func=ACT.Square, accum_out=ss[b][:, 2 * i + j:2 * i + j + 1])
+
+        def root(b):
             nc.scalar.activation(out=rr[b][:], in_=ss[b][:], func=ACT.Sqrt)
 
         def rmax(b):
@@ -162,8 +167,8 @@ def tile_gat_pa_kernel(tc, x_bytes, x_scale, W1, b1, W2, b2, W3, b3, out):
         def rcp(b):
             nc.vector.reciprocal(out=ri[b][:], in_=rm[b][:])
 
-        def scale(b, first, last, eng):
-            for k in range(first, last):
+        def scale(b, items, eng):
+            for k in items:
                 c, h = units(b)[k // 2]
                 j = k % 2
                 if eng == "S":
@@ -207,27 +212,35 @@ def tile_gat_pa_kernel(tc, x_bytes, x_scale, W1, b1, W2, b2, W3, b3, out):
         wcopy(2, 1)
         for i, b in enumerate(BATCHES):
             prev = BATCHES[i - 1] if i > 0 else None
+            prev2 = BATCHES[i - 2] if i > 1 else None
             badd(b, 0)
+            badd(b, 1)
+            if i >= 2 and i + 2 < len(BATCHES):
+                mm(BATCHES[i + 2])
+            square(b)
             if prev:
                 rmax(prev)
-            badd(b, 1)
+            if i == 1:
+                wquant(2, 0)
+            if prev2:
+                scale(prev2, (1,), "V")
             if prev:
                 rcp(prev)
             if i == 1:
-                wquant(2, 0)
                 wquant(2, 1)
                 mm(BATCHES[2])
                 xquant(3)
                 mm(BATCHES[3])
-            if i >= 2 and i + 2 < len(BATCHES):
-                mm(BATCHES[i + 2])
+            if prev2:
+                scale(prev2, (2,), "V")
             if prev:
-                scale(prev, 0, N_V_SCALE, "V")
-            square(b)
-            if prev:
-                scale(prev, N_V_SCALE, 4, "S")
+                scale(prev, (0,), "V")
+                scale(prev, (3,), "S")
+            root(b)
         last = BATCHES[-1]
+        scale(BATCHES[-2], (1,), "V")
         rmax(last)
+        scale(BATCHES[-2], (2,), "V")
         rcp(last)
-        scale(last, 0, 2, "V")
-        scale(last, 2, 4, "S")
+        scale(last, (0, 1), "V")
+        scale(last, (2, 3), "S")

@@ -186,7 +186,7 @@ def tile_gat_pa_kernel(tc, x_bytes, x_scale, W1, b1, W2, b2, W3, b3, out):
                         dummy()
         bias_matmul()
         bias_copy()
-        for h in range(2):
+        for h in range(HEADS):
             for g in range(G):
                 wtrans(h, g)
         inter(0, "V")
@@ -201,16 +201,17 @@ def tile_gat_pa_kernel(tc, x_bytes, x_scale, W1, b1, W2, b2, W3, b3, out):
         wcopy(1, 0)
         wcopy(1, 1)
         inter(2, "V")
-        inter(3, "S")
-        wtrans(2, 0)
-        wtrans(2, 1)
         wquant(1, 0)
         wquant(1, 1)
         mm(BATCHES[1])
-        xquant(2)
         wcopy(2, 0)
         wcopy(2, 1)
-        for i, b in enumerate(BATCHES):
+        inter(3, "S")
+        xquant(2)
+        wquant(2, 0)
+        wquant(2, 1)
+        mm(BATCHES[2])
+        for i, b in enumerate(BATCHES[:-1]):
             prev = BATCHES[i - 1] if i > 0 else None
             prev2 = BATCHES[i - 2] if i > 1 else None
             badd(b, 0)
@@ -221,26 +222,30 @@ def tile_gat_pa_kernel(tc, x_bytes, x_scale, W1, b1, W2, b2, W3, b3, out):
             if prev:
                 rmax(prev)
             if i == 1:
-                wquant(2, 0)
+                xquant(3)
+                mm(BATCHES[3])
             if prev2:
                 scale(prev2, (1,), "V")
             if prev:
                 rcp(prev)
-            if i == 1:
-                wquant(2, 1)
-                mm(BATCHES[2])
-                xquant(3)
-                mm(BATCHES[3])
             if prev2:
                 scale(prev2, (2,), "V")
             if prev:
                 scale(prev, (0,), "V")
                 scale(prev, (3,), "S")
             root(b)
-        last = BATCHES[-1]
-        scale(BATCHES[-2], (1,), "V")
+        prev2, prev, last = BATCHES[-3], BATCHES[-2], BATCHES[-1]
+        badd(last, 0)
+        badd(last, 1)
+        square(last)
+        root(last)
+        rmax(prev)
+        scale(prev2, (1,), "V")
+        rcp(prev)
+        scale(prev2, (2,), "V")
         rmax(last)
-        scale(BATCHES[-2], (2,), "V")
+        scale(prev, (0,), "V")
         rcp(last)
-        scale(last, (0, 1), "V")
-        scale(last, (2, 3), "S")
+        scale(prev, (3, 1, 2), "S")
+        scale(last, (0, 1, 2), "V")
+        scale(last, (3,), "S")

@@ -22,9 +22,10 @@ CH = 256
 FLOPS = 2 * NODES * FEAT * D * HEADS
 
 N_V_SCALE = 3
-N_DUMMY = 6
+N_DUMMY = 4
 BATCHES = tuple((pair, h) for pair in range(2) for h in range(HEADS))
-UNIT_BANK = (6, 0, 1, 2, 3, 4, 5, 6, 0, 1, 2, 3)
+UNIT_BANK = (0, 1, 2, 3, 4, 5, 6, 7, 0, 1, 2, 3)
+XI_BANK = (7, 6)
 DUMMY_BANK = 7
 
 
@@ -47,13 +48,15 @@ def tile_gat_pa_kernel(tc, x_bytes, x_scale, W1, b1, W2, b2, W3, b3, out):
         nc.vector.memset(ones[:], 1.0)
         ident = keep.tile([P, P], F32, name="ident")
         make_identity(nc, ident[:])
+        identb = keep.tile([P, P], BF16, name="identb")
+        make_identity(nc, identb[:])
 
         xs = keep.tile([P, G, 4], F32, name="xs")
         nc.scalar.dma_start(out=xs[:], in_=x_scale[0].rearrange("(g p t) a b -> p g (t a b)", g=G, p=P, t=4))
         for i, b in enumerate((b1, b2, b3)):
             nc.scalar.dma_start(out=brow[0:1, i * D:(i + 1) * D], in_=b.rearrange("(o d) -> o d", o=1))
         warm = keep.tile([P, 1], F32, name="warm")
-        nc.scalar.activation(out=warm[:], in_=one1[:], func=ACT.Sqrt)
+        nc.scalar.activation(out=warm[:], in_=one1[:], func=ACT.Abs_reciprocal_sqrt)
         xv = x_bytes[0].rearrange("(g p t) h w -> p g t (h w)", g=G, p=P, t=4)
         xb = {}
         for g in range(G):
@@ -78,11 +81,10 @@ def tile_gat_pa_kernel(tc, x_bytes, x_scale, W1, b1, W2, b2, W3, b3, out):
             xsc.append(keep.tile([P, G, CH], U8, name="xsc%d" % c, align_bytes=64))
             hh.append(keep.tile([P, 2, HEADS, D], F32, name="hh%d" % c))
             oo.append(keep.tile([P, 2, HEADS, D], F32, name="oo%d" % c))
-        ss, rr, rm, ri = {}, {}, {}, {}
+        ss, rr, ri = {}, {}, {}
         for b in BATCHES:
             ss[b] = keep.tile([P, 4], F32, name="ss%d%d" % b)
             rr[b] = keep.tile([P, 4], F32, name="rr%d%d" % b)
-            rm[b] = keep.tile([P, 4], F32, name="rm%d%d" % b)
             ri[b] = keep.tile([P, 4], F32, name="ri%d%d" % b)
         wt, wg, pu = {}, {}, {}
         outv = out.rearrange("h (q p) d -> h q p d", p=P)
@@ -113,6 +115,16 @@ def tile_gat_pa_kernel(tc, x_bytes, x_scale, W1, b1, W2, b2, W3, b3, out):
                 nc.scalar.copy(out=xg[c][:], in_=src)
             else:
                 nc.vector.tensor_copy(out=xg[c][:], in_=src)
+
+        def xident(c, g):
+            xp = bank(XI_BANK[g], "xi", [P, 1024], BF16)
+            pu[("xi", c, g)] = xp
+            for j in range(2):
+                n0 = (c % 2) * CH + j * P
+                nc.tensor.matmul(out=xp[:, j * 512:(j + 1) * 512], lhsT=identb[:], rhs=xw[c // 2][:, g, :, n0:n0 + P].rearrange("p t n -> p n t"), start=True, stop=True)
+
+        def xcopy(c, g):
+            nc.scalar.copy(out=xg[c][:, g, :, :].rearrange("p n t -> p (n t)"), in_=pu[("xi", c, g)][:])
 
         def xquant(c):
             nc.vector.quantize_mx(out=xq[c][:].rearrange("p g n -> p (g n)").bitcast(FP8X4), scales=xsc[c][:].rearrange("p g n -> p (g n)"), in_=xg[c][:].rearrange("p g n t -> p (g n t)"))
@@ -159,13 +171,10 @@ def tile_gat_pa_kernel(tc, x_bytes, x_scale, W1, b1, W2, b2, W3, b3, out):
                     nc.scalar.activation(out=junk[:, BATCHES.index(b), 2 * i + j, :], in_=hh[c][:, j, h, :], func=ACT.Square, accum_out=ss[b][:, 2 * i + j:2 * i + j + 1])
 
         def root(b):
-            nc.scalar.activation(out=rr[b][:], in_=ss[b][:], func=ACT.Sqrt)
+            nc.scalar.activation(out=rr[b][:], in_=ss[b][:], func=ACT.Abs_reciprocal_sqrt)
 
         def rmax(b):
-            nc.vector.tensor_scalar_max(out=rm[b][:], in0=rr[b][:], scalar1=1e-12)
-
-        def rcp(b):
-            nc.vector.reciprocal(out=ri[b][:], in_=rm[b][:])
+            nc.vector.tensor_scalar_min(out=ri[b][:], in0=rr[b][:], scalar1=1e12)
 
         def scale(b, items, eng):
             for k in items:
@@ -184,11 +193,14 @@ def tile_gat_pa_kernel(tc, x_bytes, x_scale, W1, b1, W2, b2, W3, b3, out):
                 if (g, t) == (0, 0):
                     for i in range(N_DUMMY):
                         dummy()
+                if (g, t) == (0, 3):
+                    xident(3, 0)
         bias_matmul()
         bias_copy()
         for h in range(HEADS):
             for g in range(G):
                 wtrans(h, g)
+        xident(3, 1)
         inter(0, "V")
         inter(1, "V")
         xquant(0)
@@ -206,7 +218,8 @@ def tile_gat_pa_kernel(tc, x_bytes, x_scale, W1, b1, W2, b2, W3, b3, out):
         mm(BATCHES[1])
         wcopy(2, 0)
         wcopy(2, 1)
-        inter(3, "S")
+        xcopy(3, 0)
+        xcopy(3, 1)
         xquant(2)
         wquant(2, 0)
         wquant(2, 1)
@@ -226,8 +239,6 @@ def tile_gat_pa_kernel(tc, x_bytes, x_scale, W1, b1, W2, b2, W3, b3, out):
                 mm(BATCHES[3])
             if prev2:
                 scale(prev2, (1,), "V")
-            if prev:
-                rcp(prev)
             if prev2:
                 scale(prev2, (2,), "V")
             if prev:
@@ -241,11 +252,9 @@ def tile_gat_pa_kernel(tc, x_bytes, x_scale, W1, b1, W2, b2, W3, b3, out):
         root(last)
         rmax(prev)
         scale(prev2, (1,), "V")
-        rcp(prev)
         scale(prev2, (2,), "V")
-        rmax(last)
         scale(prev, (0,), "V")
-        rcp(last)
+        rmax(last)
         scale(prev, (3, 1, 2), "S")
         scale(last, (0, 1, 2), "V")
         scale(last, (3,), "S")

@@ -110,11 +110,9 @@ def tile_gat_pa_kernel(tc, x_bytes, x_scale, W1, b1, W2, b2, W3, b3, out):
                 nc.scalar.activation(out=xw[pair][:, g, t, :], in_=src, func=ACT.Copy, scale=xs[:, g, t:t + 1])
 
         def inter(c, eng):
-            src = xw[c // 2][:, :, :, (c % 2) * CH:(c % 2 + 1) * CH].rearrange("p g t n -> p g n t")
-            if eng == "S":
-                nc.scalar.copy(out=xg[c][:], in_=src)
-            else:
-                nc.vector.tensor_copy(out=xg[c][:], in_=src)
+            for g in range(G):
+                src = xw[c // 2][:, g, :, (c % 2) * CH:(c % 2 + 1) * CH].rearrange("p t (c i) -> p c t i", i=4)
+                nc.vector.tensor_copy(out=xg[c][:, g, :, :].rearrange("p (c i) t -> p c t i", i=4), in_=src)
 
         def xident(c, g):
             xp = bank(XI_BANK[g], "xi", [P, 1024], BF16)

@@ -22,11 +22,12 @@ CH = 256
 FLOPS = 2 * NODES * FEAT * D * HEADS
 
 N_V_SCALE = 3
-N_DUMMY = 4
+N_DUMMY = 2
 BATCHES = tuple((pair, h) for pair in range(2) for h in range(HEADS))
 UNIT_BANK = (0, 1, 2, 3, 4, 5, 6, 7, 0, 1, 2, 3)
 XI_BANK = (7, 6)
 DUMMY_BANK = 7
+V_ALSO = ((0, 3), (1, 3))
 
 
 def tile_gat_pa_kernel(tc, x_bytes, x_scale, W1, b1, W2, b2, W3, b3, out):
@@ -73,7 +74,8 @@ def tile_gat_pa_kernel(tc, x_bytes, x_scale, W1, b1, W2, b2, W3, b3, out):
         wq = keep.tile([P, G, HEADS * D], U32, name="wq", align_bytes=64)
         wsc = keep.tile([P, G, HEADS * D], U8, name="wsc", align_bytes=64)
         junk = keep.tile([P, len(BATCHES), 4, D], BF16, name="junk")
-        xw = [keep.tile([P, G, 4, 2 * CH], BF16, name="xw%d" % pair) for pair in range(2)]
+        xwt = keep.tile([P, G, 4, NODES], BF16, name="xwt")
+        xw = [xwt[:, :, :, pair * 512:(pair + 1) * 512] for pair in range(2)]
         xg, xq, xsc, hh, oo = [], [], [], [], []
         for c in range(4):
             xg.append(keep.tile([P, G, CH, 4], BF16, name="xg%d" % c, align_bytes=64))
@@ -104,10 +106,13 @@ def tile_gat_pa_kernel(tc, x_bytes, x_scale, W1, b1, W2, b2, W3, b3, out):
 
         def widen(pair, g, t):
             src = xb[(g, t)][:, pair * 512:(pair + 1) * 512].bitcast(FP8)
-            if pair == 0:
+            if pair == 0 or (g, t) in V_ALSO:
                 nc.vector.tensor_scalar(out=xw[pair][:, g, t, :], in0=src, scalar1=xs[:, g, t:t + 1], scalar2=None, op0=ALU.mult)
             else:
                 nc.scalar.activation(out=xw[pair][:, g, t, :], in_=src, func=ACT.Copy, scale=xs[:, g, t:t + 1])
+
+        def widen_whole(g, t):
+            nc.vector.tensor_scalar(out=xwt[:, g, t, :], in0=xb[(g, t)][:].bitcast(FP8), scalar1=xs[:, g, t:t + 1], scalar2=None, op0=ALU.mult)
 
         def inter(c, eng):
             for g in range(G):
@@ -186,14 +191,17 @@ def tile_gat_pa_kernel(tc, x_bytes, x_scale, W1, b1, W2, b2, W3, b3, out):
 
         for g in range(G):
             for t in range(4):
-                widen(0, g, t)
-                widen(1, g, t)
+                if (g, t) in V_ALSO:
+                    widen_whole(g, t)
+                else:
+                    widen(0, g, t)
+                    widen(1, g, t)
                 if (g, t) == (0, 0):
                     for i in range(N_DUMMY):
                         dummy()
+                    bias_matmul()
                 if (g, t) == (0, 3):
                     xident(3, 0)
-        bias_matmul()
         bias_copy()
         for h in range(HEADS):
             for g in range(G):
@@ -214,19 +222,20 @@ def tile_gat_pa_kernel(tc, x_bytes, x_scale, W1, b1, W2, b2, W3, b3, out):
         wquant(1, 0)
         wquant(1, 1)
         mm(BATCHES[1])
+        xcopy(3, 0)
         wcopy(2, 0)
         wcopy(2, 1)
-        xcopy(3, 0)
         xcopy(3, 1)
-        xquant(2)
-        wquant(2, 0)
-        wquant(2, 1)
-        mm(BATCHES[2])
         for i, b in enumerate(BATCHES[:-1]):
             prev = BATCHES[i - 1] if i > 0 else None
             prev2 = BATCHES[i - 2] if i > 1 else None
             badd(b, 0)
             badd(b, 1)
+            if i == 0:
+                xquant(2)
+                wquant(2, 0)
+                wquant(2, 1)
+                mm(BATCHES[2])
             if i >= 2 and i + 2 < len(BATCHES):
                 mm(BATCHES[i + 2])
             square(b)

@@ -54,8 +54,6 @@ def tile_gat_pa_kernel(tc, x_bytes, x_scale, W1, b1, W2, b2, W3, b3, out):
 
         xs = keep.tile([P, G, 4], F32, name="xs")
         nc.scalar.dma_start(out=xs[:], in_=x_scale[0].rearrange("(g p t) a b -> p g (t a b)", g=G, p=P, t=4))
-        for i, b in enumerate((b1, b2, b3)):
-            nc.scalar.dma_start(out=brow[0:1, i * D:(i + 1) * D], in_=b.rearrange("(o d) -> o d", o=1))
         warm = keep.tile([P, 1], F32, name="warm")
         nc.scalar.activation(out=warm[:], in_=one1[:], func=ACT.Abs_reciprocal_sqrt)
         xv = x_bytes[0].rearrange("(g p t) h w -> p g t (h w)", g=G, p=P, t=4)
@@ -64,6 +62,8 @@ def tile_gat_pa_kernel(tc, x_bytes, x_scale, W1, b1, W2, b2, W3, b3, out):
             for t in range(4):
                 xb[(g, t)] = keep.tile([P, NODES], U8, name="xb%d%d" % (g, t))
                 nc.sync.dma_start(out=xb[(g, t)][:], in_=xv[:, g, t, :])
+        for i, b in enumerate((b1, b2, b3)):
+            nc.sync.dma_start(out=brow[0:1, i * D:(i + 1) * D], in_=b.rearrange("(o d) -> o d", o=1))
         wraw = []
         for h in range(HEADS):
             wr = keep.tile([P, 2, FEAT], BF16, name="wraw%d" % h)
@@ -74,8 +74,10 @@ def tile_gat_pa_kernel(tc, x_bytes, x_scale, W1, b1, W2, b2, W3, b3, out):
         wq = keep.tile([P, G, HEADS * D], U32, name="wq", align_bytes=64)
         wsc = keep.tile([P, G, HEADS * D], U8, name="wsc", align_bytes=64)
         junk = keep.tile([P, len(BATCHES), 4, D], BF16, name="junk")
-        xwt = keep.tile([P, G, 4, NODES], BF16, name="xwt")
-        xw = [xwt[:, :, :, pair * 512:(pair + 1) * 512] for pair in range(2)]
+        xw = []
+        for pair in range(2):
+            xwp = keep.tile([P, G, 4, 512], BF16, name="xw%d" % pair)
+            xw.append(xwp)
         xg, xq, xsc, hh, oo = [], [], [], [], []
         for c in range(4):
             xg.append(keep.tile([P, G, CH, 4], BF16, name="xg%d" % c, align_bytes=64))
@@ -110,9 +112,6 @@ def tile_gat_pa_kernel(tc, x_bytes, x_scale, W1, b1, W2, b2, W3, b3, out):
                 nc.vector.tensor_scalar(out=xw[pair][:, g, t, :], in0=src, scalar1=xs[:, g, t:t + 1], scalar2=None, op0=ALU.mult)
             else:
                 nc.scalar.activation(out=xw[pair][:, g, t, :], in_=src, func=ACT.Copy, scale=xs[:, g, t:t + 1])
-
-        def widen_whole(g, t):
-            nc.vector.tensor_scalar(out=xwt[:, g, t, :], in0=xb[(g, t)][:].bitcast(FP8), scalar1=xs[:, g, t:t + 1], scalar2=None, op0=ALU.mult)
 
         def inter(c, eng):
             for g in range(G):
@@ -191,16 +190,13 @@ def tile_gat_pa_kernel(tc, x_bytes, x_scale, W1, b1, W2, b2, W3, b3, out):
 
         for g in range(G):
             for t in range(4):
-                if (g, t) in V_ALSO:
-                    widen_whole(g, t)
-                else:
-                    widen(0, g, t)
-                    widen(1, g, t)
+                widen(0, g, t)
+                widen(1, g, t)
                 if (g, t) == (0, 0):
                     for i in range(N_DUMMY):
                         dummy()
-                    bias_matmul()
                 if (g, t) == (0, 3):
+                    bias_matmul()
                     xident(3, 0)
         bias_copy()
         for h in range(HEADS):

@@ -28,6 +28,7 @@ UNIT_BANK = (0, 1, 2, 3, 4, 5, 6, 7, 0, 1, 2, 3)
 XI_BANK = (7, 6)
 DUMMY_BANK = 7
 V_ALSO = ((0, 3), (1, 3))
+X_LOADS = ((0, 0, 1), (0, 1, 2), (0, 2, 4), (1, 0, 2), (1, 2, 4))
 
 
 def tile_gat_pa_kernel(tc, x_bytes, x_scale, W1, b1, W2, b2, W3, b3, out):
@@ -43,8 +44,6 @@ def tile_gat_pa_kernel(tc, x_bytes, x_scale, W1, b1, W2, b2, W3, b3, out):
 
         one1 = keep.tile([P, 1], F32, name="one1")
         nc.vector.memset(one1[:], 1.0)
-        brow = keep.tile([P, HEADS * D], BF16, name="brow")
-        nc.vector.memset(brow[:], 0.0)
         ones = keep.tile([P, P], BF16, name="ones")
         nc.vector.memset(ones[:], 1.0)
         ident = keep.tile([P, P], F32, name="ident")
@@ -54,16 +53,20 @@ def tile_gat_pa_kernel(tc, x_bytes, x_scale, W1, b1, W2, b2, W3, b3, out):
 
         xs = keep.tile([P, G, 4], F32, name="xs")
         nc.scalar.dma_start(out=xs[:], in_=x_scale[0].rearrange("(g p t) a b -> p g (t a b)", g=G, p=P, t=4))
+        bcol = []
+        for i, b in enumerate((b1, b2, b3)):
+            bc = keep.tile([P, 2], BF16, name="bcol%d" % i)
+            nc.scalar.dma_start(out=bc[:], in_=b.rearrange("(p e) -> p e", e=2))
+            bcol.append(bc)
         warm = keep.tile([P, 1], F32, name="warm")
         nc.scalar.activation(out=warm[:], in_=one1[:], func=ACT.Abs_reciprocal_sqrt)
         xv = x_bytes[0].rearrange("(g p t) h w -> p g t (h w)", g=G, p=P, t=4)
         xb = {}
-        for g in range(G):
-            for t in range(4):
-                xb[(g, t)] = keep.tile([P, NODES], U8, name="xb%d%d" % (g, t))
-                nc.sync.dma_start(out=xb[(g, t)][:], in_=xv[:, g, t, :])
-        for i, b in enumerate((b1, b2, b3)):
-            nc.sync.dma_start(out=brow[0:1, i * D:(i + 1) * D], in_=b.rearrange("(o d) -> o d", o=1))
+        for g, lo, hi in X_LOADS:
+            xt = keep.tile([P, hi - lo, NODES], U8, name="xb%d%d" % (g, lo))
+            nc.sync.dma_start(out=xt[:], in_=xv[:, g, lo:hi, :])
+            for t in range(lo, hi):
+                xb[(g, t)] = xt[:, t - lo, :]
         wraw = []
         for h in range(HEADS):
             wr = keep.tile([P, 2, FEAT], BF16, name="wraw%d" % h)
@@ -100,11 +103,12 @@ def tile_gat_pa_kernel(tc, x_bytes, x_scale, W1, b1, W2, b2, W3, b3, out):
         def bias_matmul():
             bp = bank(6, "bp", [P, 1024], BF16)
             pu["bias"] = bp
-            nc.tensor.matmul(out=bp[:, 0:512], lhsT=ones[:], rhs=brow[:, 0:512], start=True, stop=True)
-            nc.tensor.matmul(out=bp[:, 512:768], lhsT=ones[:], rhs=brow[:, 512:768], start=True, stop=True)
+            for i in range(HEADS):
+                for e in range(2):
+                    nc.tensor.matmul(out=bp[:, i * D + e * P:i * D + (e + 1) * P], lhsT=bcol[i][:, e:e + 1].to_broadcast([P, P]), rhs=identb[:], start=True, stop=True)
 
         def bias_copy():
-            nc.scalar.copy(out=bias[:], in_=pu["bias"][:, 0:768])
+            nc.scalar.copy(out=bias[:].rearrange("p (h n e) -> p h n e", h=HEADS, e=2), in_=pu["bias"][:, 0:768].rearrange("p (h e n) -> p h n e", h=HEADS, e=2))
 
         def widen(pair, g, t):
             src = xb[(g, t)][:, pair * 512:(pair + 1) * 512].bitcast(FP8)

@@ -22,13 +22,10 @@ CH = 256
 FLOPS = 2 * NODES * FEAT * D * HEADS
 
 N_V_SCALE = 3
-N_DUMMY = 2
 BATCHES = tuple((pair, h) for pair in range(2) for h in range(HEADS))
 UNIT_BANK = (0, 1, 2, 3, 4, 5, 6, 7, 0, 1, 2, 3)
 XI_BANK = (7, 6)
-DUMMY_BANK = 7
-V_ALSO = ((0, 3), (1, 3))
-X_LOADS = ((0, 0, 1), (0, 1, 2), (0, 2, 4), (1, 0, 2), (1, 2, 4))
+V_ALSO = ((1, 3),)
 
 
 def tile_gat_pa_kernel(tc, x_bytes, x_scale, W1, b1, W2, b2, W3, b3, out):
@@ -46,10 +43,10 @@ def tile_gat_pa_kernel(tc, x_bytes, x_scale, W1, b1, W2, b2, W3, b3, out):
         nc.vector.memset(one1[:], 1.0)
         ones = keep.tile([P, P], BF16, name="ones")
         nc.vector.memset(ones[:], 1.0)
-        ident = keep.tile([P, P], F32, name="ident")
-        make_identity(nc, ident[:])
         identb = keep.tile([P, P], BF16, name="identb")
         make_identity(nc, identb[:])
+        ident = keep.tile([P, P], F32, name="ident")
+        make_identity(nc, ident[:])
 
         xs = keep.tile([P, G, 4], F32, name="xs")
         nc.scalar.dma_start(out=xs[:], in_=x_scale[0].rearrange("(g p t) a b -> p g (t a b)", g=G, p=P, t=4))
@@ -61,17 +58,26 @@ def tile_gat_pa_kernel(tc, x_bytes, x_scale, W1, b1, W2, b2, W3, b3, out):
         warm = keep.tile([P, 1], F32, name="warm")
         nc.scalar.activation(out=warm[:], in_=one1[:], func=ACT.Abs_reciprocal_sqrt)
         xv = x_bytes[0].rearrange("(g p t) h w -> p g t (h w)", g=G, p=P, t=4)
-        xb = {}
-        for g, lo, hi in X_LOADS:
+        xb, wraw = {}, {}
+
+        def load_x(g, lo, hi):
             xt = keep.tile([P, hi - lo, NODES], U8, name="xb%d%d" % (g, lo))
             nc.sync.dma_start(out=xt[:], in_=xv[:, g, lo:hi, :])
             for t in range(lo, hi):
                 xb[(g, t)] = xt[:, t - lo, :]
-        wraw = []
-        for h in range(HEADS):
-            wr = keep.tile([P, 2, FEAT], BF16, name="wraw%d" % h)
-            nc.sync.dma_start(out=wr[:], in_=Ws[h].rearrange("(a p) k -> p a k", p=P))
-            wraw.append(wr)
+
+        def load_w(h):
+            wraw[h] = keep.tile([P, 2, FEAT], BF16, name="wraw%d" % h)
+            nc.sync.dma_start(out=wraw[h][:], in_=Ws[h].rearrange("(a p) k -> p a k", p=P))
+
+        load_x(0, 0, 1)
+        load_x(0, 1, 2)
+        load_x(0, 2, 4)
+        load_w(0)
+        load_x(1, 0, 2)
+        load_x(1, 2, 4)
+        load_w(1)
+        load_w(2)
 
         bias = keep.tile([P, HEADS * D], BF16, name="bias")
         wq = keep.tile([P, G, HEADS * D], U32, name="wq", align_bytes=64)
@@ -96,12 +102,12 @@ def tile_gat_pa_kernel(tc, x_bytes, x_scale, W1, b1, W2, b2, W3, b3, out):
         wt, wg, pu = {}, {}, {}
         outv = out.rearrange("h (q p) d -> h q p d", p=P)
 
-        def dummy():
-            dm = bank(DUMMY_BANK, "dm", [P, 512], F32)
+        def dummy(k):
+            dm = bank(k, "dm", [P, 512], F32)
             nc.tensor.matmul(out=dm[:], lhsT=ones[:], rhs=xw[0][:, 0, 0, :], start=True, stop=True)
 
         def bias_matmul():
-            bp = bank(6, "bp", [P, 1024], BF16)
+            bp = bank(5, "bp", [P, 1024], BF16)
             pu["bias"] = bp
             for i in range(HEADS):
                 for e in range(2):
@@ -117,10 +123,9 @@ def tile_gat_pa_kernel(tc, x_bytes, x_scale, W1, b1, W2, b2, W3, b3, out):
             else:
                 nc.scalar.activation(out=xw[pair][:, g, t, :], in_=src, func=ACT.Copy, scale=xs[:, g, t:t + 1])
 
-        def inter(c, eng):
-            for g in range(G):
-                src = xw[c // 2][:, g, :, (c % 2) * CH:(c % 2 + 1) * CH].rearrange("p t (c i) -> p c t i", i=4)
-                nc.vector.tensor_copy(out=xg[c][:, g, :, :].rearrange("p (c i) t -> p c t i", i=4), in_=src)
+        def inter(c, g):
+            src = xw[c // 2][:, g, :, (c % 2) * CH:(c % 2 + 1) * CH].rearrange("p t (c i) -> p c t i", i=4)
+            nc.vector.tensor_copy(out=xg[c][:, g, :, :].rearrange("p (c i) t -> p c t i", i=4), in_=src)
 
         def xident(c, g):
             xp = bank(XI_BANK[g], "xi", [P, 1024], BF16)
@@ -192,37 +197,46 @@ def tile_gat_pa_kernel(tc, x_bytes, x_scale, W1, b1, W2, b2, W3, b3, out):
                     nc.vector.tensor_scalar(out=oo[c][:, j, h, :], in0=hh[c][:, j, h, :], scalar1=ri[b][:, k:k + 1], scalar2=None, op0=ALU.mult)
                 nc.sync.dma_start(out=outv[h, 2 * c + j], in_=oo[c][:, j, h, :])
 
-        for g in range(G):
-            for t in range(4):
-                widen(0, g, t)
-                widen(1, g, t)
-                if (g, t) == (0, 0):
-                    for i in range(N_DUMMY):
-                        dummy()
-                if (g, t) == (0, 3):
-                    bias_matmul()
-                    xident(3, 0)
-        bias_copy()
-        for h in range(HEADS):
-            for g in range(G):
-                wtrans(h, g)
+        bias_matmul()
+        for t in range(4):
+            widen(0, 0, t)
+            widen(1, 0, t)
+            if t == 0:
+                dummy(7)
+                dummy(7)
+        wtrans(0, 0)
+        wtrans(0, 1)
+        xident(3, 0)
+        inter(0, 0)
+        inter(1, 0)
+        for t in range(4):
+            widen(0, 1, t)
+            widen(1, 1, t)
+        dummy(6)
+        wtrans(1, 0)
+        wtrans(1, 1)
         xident(3, 1)
-        inter(0, "V")
-        inter(1, "V")
+        inter(0, 1)
+        inter(1, 1)
         xquant(0)
         xquant(1)
+        bias_copy()
         wcopy(0, 0)
         wcopy(0, 1)
+        wtrans(2, 0)
+        wtrans(2, 1)
+        dummy(0)
         wquant(0, 0)
         wquant(0, 1)
-        mm(BATCHES[0])
         wcopy(1, 0)
         wcopy(1, 1)
-        inter(2, "V")
+        mm(BATCHES[0])
+        xcopy(3, 0)
+        inter(2, 0)
+        inter(2, 1)
         wquant(1, 0)
         wquant(1, 1)
         mm(BATCHES[1])
-        xcopy(3, 0)
         wcopy(2, 0)
         wcopy(2, 1)
         xcopy(3, 1)

@@ -50,11 +50,6 @@ def tile_gat_pa_kernel(tc, x_bytes, x_scale, W1, b1, W2, b2, W3, b3, out):
 
         xs = keep.tile([P, G, 4], F32, name="xs")
         nc.scalar.dma_start(out=xs[:], in_=x_scale[0].rearrange("(g p t) a b -> p g (t a b)", g=G, p=P, t=4))
-        bcol = []
-        for i, b in enumerate((b1, b2, b3)):
-            bc = keep.tile([P, 2], BF16, name="bcol%d" % i)
-            nc.scalar.dma_start(out=bc[:], in_=b.rearrange("(p e) -> p e", e=2))
-            bcol.append(bc)
         warm = keep.tile([P, 1], F32, name="warm")
         nc.scalar.activation(out=warm[:], in_=one1[:], func=ACT.Abs_reciprocal_sqrt)
         xv = x_bytes[0].rearrange("(g p t) h w -> p g t (h w)", g=G, p=P, t=4)
@@ -77,6 +72,11 @@ def tile_gat_pa_kernel(tc, x_bytes, x_scale, W1, b1, W2, b2, W3, b3, out):
         load_x(1, 0, 2)
         load_x(1, 2, 4)
         load_w(1)
+        bcol = []
+        for i, b in enumerate((b1, b2, b3)):
+            bc = keep.tile([P, 2], BF16, name="bcol%d" % i)
+            nc.sync.dma_start(out=bc[:], in_=b.rearrange("(p e) -> p e", e=2))
+            bcol.append(bc)
         load_w(2)
 
         bias = keep.tile([P, HEADS * D], BF16, name="bias")
@@ -107,7 +107,7 @@ def tile_gat_pa_kernel(tc, x_bytes, x_scale, W1, b1, W2, b2, W3, b3, out):
             nc.tensor.matmul(out=dm[:], lhsT=ones[:], rhs=xw[0][:, 0, 0, :], start=True, stop=True)
 
         def bias_matmul():
-            bp = bank(5, "bp", [P, 1024], BF16)
+            bp = bank(7, "bp", [P, 1024], BF16)
             pu["bias"] = bp
             for i in range(HEADS):
                 for e in range(2):
@@ -173,19 +173,24 @@ def tile_gat_pa_kernel(tc, x_bytes, x_scale, W1, b1, W2, b2, W3, b3, out):
             c, h = units(b)[i]
             nc.vector.tensor_tensor(out=hh[c][:, :, h, :], in0=pu[(c, h)][:], in1=bias[:, h * D:(h + 1) * D].unsqueeze(1).to_broadcast([P, 2, D]), op=ALU.add)
 
+        def square_tile(b, k, eng):
+            c, h = units(b)[k // 2]
+            tile_h = hh[c][:, k % 2, h, :]
+            dump = junk[:, BATCHES.index(b), k, :]
+            if eng == "S":
+                nc.scalar.activation(out=dump, in_=tile_h, func=ACT.Square, accum_out=ss[b][:, k:k + 1])
+            else:
+                nc.vector.scalar_tensor_tensor(out=dump, in0=tile_h, scalar=1.0, in1=tile_h, op0=ALU.mult, op1=ALU.mult, accum_out=ss[b][:, k:k + 1])
+
         def square(b):
-            for i, (c, h) in enumerate(units(b)):
-                for j in range(2):
-                    if b == BATCHES[-1] and (i, j) == (1, 1):
-                        nc.vector.scalar_tensor_tensor(out=junk[:, BATCHES.index(b), 3, :], in0=hh[c][:, j, h, :], scalar=1.0, in1=hh[c][:, j, h, :], op0=ALU.mult, op1=ALU.mult, accum_out=ss[b][:, 3:4])
-                        continue
-                    nc.scalar.activation(out=junk[:, BATCHES.index(b), 2 * i + j, :], in_=hh[c][:, j, h, :], func=ACT.Square, accum_out=ss[b][:, 2 * i + j:2 * i + j + 1])
+            for k in range(4):
+                square_tile(b, k, "S")
 
-        def root(b):
-            nc.scalar.activation(out=rr[b][:], in_=ss[b][:], func=ACT.Abs_reciprocal_sqrt)
+        def root(b, lo=0, hi=4):
+            nc.scalar.activation(out=rr[b][:, lo:hi], in_=ss[b][:, lo:hi], func=ACT.Abs_reciprocal_sqrt)
 
-        def rmax(b):
-            nc.vector.tensor_scalar_min(out=ri[b][:], in0=rr[b][:], scalar1=1e12)
+        def rmax(b, lo=0, hi=4):
+            nc.vector.tensor_scalar_min(out=ri[b][:, lo:hi], in0=rr[b][:, lo:hi], scalar1=1e12)
 
         def scale(b, items, eng):
             for k in items:
@@ -195,9 +200,14 @@ def tile_gat_pa_kernel(tc, x_bytes, x_scale, W1, b1, W2, b2, W3, b3, out):
                     nc.scalar.activation(out=oo[c][:, j, h, :], in_=hh[c][:, j, h, :], func=ACT.Copy, scale=ri[b][:, k:k + 1])
                 else:
                     nc.vector.tensor_scalar(out=oo[c][:, j, h, :], in0=hh[c][:, j, h, :], scalar1=ri[b][:, k:k + 1], scalar2=None, op0=ALU.mult)
-                nc.sync.dma_start(out=outv[h, 2 * c + j], in_=oo[c][:, j, h, :])
+                if eng == "V":
+                    store(b, (k,))
 
-        bias_matmul()
+        def store(b, items):
+            for k in items:
+                c, h = units(b)[k // 2]
+                nc.sync.dma_start(out=outv[h, 2 * c + k % 2], in_=oo[c][:, k % 2, h, :])
+
         for t in range(4):
             widen(0, 0, t)
             widen(1, 0, t)
@@ -220,18 +230,18 @@ def tile_gat_pa_kernel(tc, x_bytes, x_scale, W1, b1, W2, b2, W3, b3, out):
         inter(1, 1)
         xquant(0)
         xquant(1)
-        bias_copy()
         wcopy(0, 0)
         wcopy(0, 1)
+        xcopy(3, 0)
+        bias_matmul()
         wtrans(2, 0)
         wtrans(2, 1)
-        dummy(0)
         wquant(0, 0)
         wquant(0, 1)
         wcopy(1, 0)
         wcopy(1, 1)
         mm(BATCHES[0])
-        xcopy(3, 0)
+        bias_copy()
         inter(2, 0)
         inter(2, 1)
         wquant(1, 0)
@@ -259,23 +269,31 @@ def tile_gat_pa_kernel(tc, x_bytes, x_scale, W1, b1, W2, b2, W3, b3, out):
                 xquant(3)
                 mm(BATCHES[3])
             if prev2:
-                scale(prev2, (1,), "V")
-            if prev2:
                 scale(prev2, (2,), "V")
             if prev:
-                scale(prev, (0,), "V")
+                scale(prev, (0, 1), "V")
                 scale(prev, (3,), "S")
+                store(prev, (3,))
             root(b)
         prev2, prev, last = BATCHES[-3], BATCHES[-2], BATCHES[-1]
         badd(last, 0)
         badd(last, 1)
-        square(last)
-        root(last)
+        square_tile(last, 0, "S")
+        square_tile(last, 1, "S")
+        square_tile(last, 2, "S")
         rmax(prev)
-        scale(prev2, (1,), "V")
         scale(prev2, (2,), "V")
+        root(last, 0, 2)
         scale(prev, (0,), "V")
-        rmax(last)
-        scale(prev, (3, 1, 2), "S")
-        scale(last, (0, 1, 2), "V")
+        scale(prev, (3,), "S")
+        square_tile(last, 3, "V")
+        root(last, 2, 4)
+        scale(prev, (1,), "V")
+        scale(prev, (2,), "V")
+        store(prev, (3,))
+        rmax(last, 0, 2)
+        rmax(last, 2, 4)
+        scale(last, (0,), "V")
         scale(last, (3,), "S")
+        scale(last, (1, 2), "V")
+        store(last, (3,))

@@ -25,7 +25,7 @@ N_V_SCALE = 3
 BATCHES = tuple((pair, h) for pair in range(2) for h in range(HEADS))
 UNIT_BANK = (0, 1, 2, 3, 4, 5, 6, 7, 0, 1, 2, 3)
 XI_BANK = (7, 6)
-V_ALSO = ((1, 3),)
+V_ALSO = ((0, 3), (1, 3))
 
 
 def tile_gat_pa_kernel(tc, x_bytes, x_scale, W1, b1, W2, b2, W3, b3, out):
@@ -55,22 +55,18 @@ def tile_gat_pa_kernel(tc, x_bytes, x_scale, W1, b1, W2, b2, W3, b3, out):
         xv = x_bytes[0].rearrange("(g p t) h w -> p g t (h w)", g=G, p=P, t=4)
         xb, wraw = {}, {}
 
-        def load_x(g, lo, hi):
-            xt = keep.tile([P, hi - lo, NODES], U8, name="xb%d%d" % (g, lo))
-            nc.sync.dma_start(out=xt[:], in_=xv[:, g, lo:hi, :])
-            for t in range(lo, hi):
-                xb[(g, t)] = xt[:, t - lo, :]
+        def load_x(g, t):
+            xb[(g, t)] = keep.tile([P, NODES], U8, name="xb%d%d" % (g, t))
+            nc.sync.dma_start(out=xb[(g, t)][:], in_=xv[:, g, t, :])
 
         def load_w(h):
             wraw[h] = keep.tile([P, 2, FEAT], BF16, name="wraw%d" % h)
             nc.sync.dma_start(out=wraw[h][:], in_=Ws[h].rearrange("(a p) k -> p a k", p=P))
 
-        load_x(0, 0, 1)
-        load_x(0, 1, 2)
-        load_x(0, 2, 4)
+        for g in range(G):
+            for t in range(4):
+                load_x(g, t)
         load_w(0)
-        load_x(1, 0, 2)
-        load_x(1, 2, 4)
         load_w(1)
         bcol = []
         for i, b in enumerate((b1, b2, b3)):
@@ -208,32 +204,30 @@ def tile_gat_pa_kernel(tc, x_bytes, x_scale, W1, b1, W2, b2, W3, b3, out):
                 c, h = units(b)[k // 2]
                 nc.sync.dma_start(out=outv[h, 2 * c + k % 2], in_=oo[c][:, k % 2, h, :])
 
-        for t in range(4):
-            widen(0, 0, t)
-            widen(1, 0, t)
-            if t == 0:
-                dummy(7)
-                dummy(7)
+        for g in range(G):
+            for t in range(4):
+                widen(0, g, t)
+                widen(1, g, t)
+                if (g, t) == (0, 0):
+                    dummy(7)
+                    dummy(7)
+            if g == 0:
+                xident(3, 0)
         wtrans(0, 0)
         wtrans(0, 1)
-        xident(3, 0)
-        inter(0, 0)
-        inter(1, 0)
-        for t in range(4):
-            widen(0, 1, t)
-            widen(1, 1, t)
-        dummy(6)
         wtrans(1, 0)
         wtrans(1, 1)
-        xident(3, 1)
+        inter(0, 0)
         inter(0, 1)
+        inter(1, 0)
         inter(1, 1)
         xquant(0)
         xquant(1)
+        xcopy(3, 0)
         wcopy(0, 0)
         wcopy(0, 1)
-        xcopy(3, 0)
         bias_matmul()
+        xident(3, 1)
         wtrans(2, 0)
         wtrans(2, 1)
         wquant(0, 0)

@@ -25,7 +25,7 @@ N_V_SCALE = 3
 BATCHES = tuple((pair, h) for pair in range(2) for h in range(HEADS))
 UNIT_BANK = (0, 1, 2, 3, 4, 5, 6, 7, 0, 1, 2, 3)
 XI_BANK = (7, 6)
-V_ALSO = ((0, 3), (1, 3))
+V_ALSO = ((0, 3),)
 
 
 def tile_gat_pa_kernel(tc, x_bytes, x_scale, W1, b1, W2, b2, W3, b3, out):
@@ -263,9 +263,9 @@ def tile_gat_pa_kernel(tc, x_bytes, x_scale, W1, b1, W2, b2, W3, b3, out):
                 xquant(3)
                 mm(BATCHES[3])
             if prev2:
-                scale(prev2, (2,), "V")
+                scale(prev2, (1, 2), "V")
             if prev:
-                scale(prev, (0, 1), "V")
+                scale(prev, (0,), "V")
                 scale(prev, (3,), "S")
                 store(prev, (3,))
             root(b)
@@ -276,7 +276,7 @@ def tile_gat_pa_kernel(tc, x_bytes, x_scale, W1, b1, W2, b2, W3, b3, out):
         square_tile(last, 1, "S")
         square_tile(last, 2, "S")
         rmax(prev)
-        scale(prev2, (2,), "V")
+        scale(prev2, (1, 2), "V")
         root(last, 0, 2)
         scale(prev, (0,), "V")
         scale(prev, (3,), "S")

from contextlib import ExitStack

import concourse.mybir as mybir
from concourse.masks import make_identity

F32 = mybir.dt.float32
BF16 = mybir.dt.bfloat16
U32 = mybir.dt.uint32
U8 = mybir.dt.uint8
FP8 = mybir.dt.float8_e4m3fn
FP8X4 = mybir.dt.float8_e4m3fn_x4
ACT = mybir.ActivationFunctionType
ALU = mybir.AluOpType

P = 128
NODES = 1024
FEAT = 1024
D = 256
HEADS = 3
G = 2
CH = 256
FLOPS = 2 * NODES * FEAT * D * HEADS

N_V_SCALE = 3
BATCHES = tuple((pair, h) for pair in range(2) for h in range(HEADS))
UNIT_BANK = (0, 1, 2, 3, 4, 5, 6, 7, 0, 1, 2, 3)
XI_BANK = (7, 6)
V_ALSO = ((0, 3),)


def tile_gat_pa_kernel(tc, x_bytes, x_scale, W1, b1, W2, b2, W3, b3, out):
    nc = tc.nc
    Ws = (W1, W2, W3)
    with ExitStack() as ctx:
        keep = ctx.enter_context(tc.tile_pool(name="keep", bufs=1))
        psum = ctx.enter_context(tc.psum_pool(name="psum", bufs=1))
        ctx.enter_context(tc.manual_schedule())

        def bank(k, name, shape, dtype):
            return psum.tile(shape, dtype, name=name, tag="bank%d" % k)

        one1 = keep.tile([P, 1], F32, name="one1")
        nc.vector.memset(one1[:], 1.0)
        ones = keep.tile([P, P], BF16, name="ones")
        nc.vector.memset(ones[:], 1.0)
        identb = keep.tile([P, P], BF16, name="identb")
        make_identity(nc, identb[:])
        ident = keep.tile([P, P], F32, name="ident")
        make_identity(nc, ident[:])

        xs = keep.tile([P, G, 4], F32, name="xs")
        nc.scalar.dma_start(out=xs[:], in_=x_scale[0].rearrange("(g p t) a b -> p g (t a b)", g=G, p=P, t=4))
        warm = keep.tile([P, 1], F32, name="warm")
        nc.scalar.activation(out=warm[:], in_=one1[:], func=ACT.Abs_reciprocal_sqrt)
        xv = x_bytes[0].rearrange("(g p t) h w -> p g t (h w)", g=G, p=P, t=4)
        xb, wraw = {}, {}

        def load_x(g, t):
            xb[(g, t)] = keep.tile([P, NODES], U8, name="xb%d%d" % (g, t))
            nc.sync.dma_start(out=xb[(g, t)][:], in_=xv[:, g, t, :])

        def load_w(h):
            wraw[h] = keep.tile([P, 2, FEAT], BF16, name="wraw%d" % h)
            nc.sync.dma_start(out=wraw[h][:], in_=Ws[h].rearrange("(a p) k -> p a k", p=P))

        for g in range(G):
            for t in range(4):
                load_x(g, t)
        load_w(0)
        load_w(1)
        bcol = []
        for i, b in enumerate((b1, b2, b3)):
            bc = keep.tile([P, 2], BF16, name="bcol%d" % i)
            nc.sync.dma_start(out=bc[:], in_=b.rearrange("(p e) -> p e", e=2))
            bcol.append(bc)
        load_w(2)

        bias = keep.tile([P, HEADS * D], BF16, name="bias")
        wq = keep.tile([P, G, HEADS * D], U32, name="wq", align_bytes=64)
        wsc = keep.tile([P, G, HEADS * D], U8, name="wsc", align_bytes=64)
        junk = keep.tile([P, len(BATCHES), 4, D], BF16, name="junk")
        xw = []
        for pair in range(2):
            xwp = keep.tile([P, G, 4, 512], BF16, name="xw%d" % pair)
            xw.append(xwp)
        xg, xq, xsc, hh, oo = [], [], [], [], []
        for c in range(4):
            xg.append(keep.tile([P, G, CH, 4], BF16, name="xg%d" % c, align_bytes=64))
            xq.append(keep.tile([P, G, CH], U32, name="xq%d" % c, align_bytes=64))
            xsc.append(keep.tile([P, G, CH], U8, name="xsc%d" % c, align_bytes=64))
            hh.append(keep.tile([P, 2, HEADS, D], F32, name="hh%d" % c))
            oo.append(keep.tile([P, 2, HEADS, D], F32, name="oo%d" % c))
        ss, rr, ri = {}, {}, {}
        for b in BATCHES:
            ss[b] = keep.tile([P, 4], F32, name="ss%d%d" % b)
            rr[b] = keep.tile([P, 4], F32, name="rr%d%d" % b)
            ri[b] = keep.tile([P, 4], F32, name="ri%d%d" % b)
        wt, wg, pu = {}, {}, {}
        outv = out.rearrange("h (q p) d -> h q p d", p=P)

        def dummy(k):
            dm = bank(k, "dm", [P, 512], F32)
            nc.tensor.matmul(out=dm[:], lhsT=ones[:], rhs=xw[0][:, 0, 0, :], start=True, stop=True)

        def bias_matmul():
            bp = bank(7, "bp", [P, 1024], BF16)
            pu["bias"] = bp
            for i in range(HEADS):
                for e in range(2):
                    nc.tensor.matmul(out=bp[:, i * D + e * P:i * D + (e + 1) * P], lhsT=bcol[i][:, e:e + 1].to_broadcast([P, P]), rhs=identb[:], start=True, stop=True)

        def bias_copy():
            nc.scalar.copy(out=bias[:].rearrange("p (h n e) -> p h n e", h=HEADS, e=2), in_=pu["bias"][:, 0:768].rearrange("p (h e n) -> p h n e", h=HEADS, e=2))

        def widen(pair, g, t):
            src = xb[(g, t)][:, pair * 512:(pair + 1) * 512].bitcast(FP8)
            if pair == 0 or (g, t) in V_ALSO:
                nc.vector.tensor_scalar(out=xw[pair][:, g, t, :], in0=src, scalar1=xs[:, g, t:t + 1], scalar2=None, op0=ALU.mult)
            else:
                nc.scalar.activation(out=xw[pair][:, g, t, :], in_=src, func=ACT.Copy, scale=xs[:, g, t:t + 1])

        def inter(c, g):
            src = xw[c // 2][:, g, :, (c % 2) * CH:(c % 2 + 1) * CH].rearrange("p t (c i) -> p c t i", i=4)
            nc.vector.tensor_copy(out=xg[c][:, g, :, :].rearrange("p (c i) t -> p c t i", i=4), in_=src)

        def xident(c, g):
            xp = bank(XI_BANK[g], "xi", [P, 1024], BF16)
            pu[("xi", c, g)] = xp
            for j in range(2):
                n0 = (c % 2) * CH + j * P
                nc.tensor.matmul(out=xp[:, j * 512:(j + 1) * 512], lhsT=identb[:], rhs=xw[c // 2][:, g, :, n0:n0 + P].rearrange("p t n -> p n t"), start=True, stop=True)

        def xcopy(c, g):
            nc.scalar.copy(out=xg[c][:, g, :, :].rearrange("p n t -> p (n t)"), in_=pu[("xi", c, g)][:])

        def xquant(c):
            nc.vector.quantize_mx(out=xq[c][:].rearrange("p g n -> p (g n)").bitcast(FP8X4), scales=xsc[c][:].rearrange("p g n -> p (g n)"), in_=xg[c][:].rearrange("p g n t -> p (g n t)"))

        def wtrans(h, g):
            words = wraw[h][:].rearrange("p a k -> p (a k)").bitcast(F32)
            w = bank(2 * h + g, "wt", [P, 512], F32)
            wt[(h, g)] = w
            for a in range(2):
                for u in range(2):
                    base = a * 512 + g * 256
                    nc.tensor.transpose(out=w[:, u * D + a * P:u * D + (a + 1) * P], in_=words[:, base + u:base + 256:2], identity=ident[:])

        def wcopy(h, g):
            wg[(h, g)] = keep.tile([P, 4 * D], BF16, name="wg%d%d" % (h, g), align_bytes=64)
            nc.scalar.copy(out=wg[(h, g)][:].bitcast(F32).rearrange("p (c u) -> p c u", u=2), in_=wt[(h, g)][:].rearrange("p (u c) -> p c u", u=2))

        def wquant(h, g):
            nc.vector.quantize_mx(out=wq[:, g, h * D:(h + 1) * D].bitcast(FP8X4), scales=wsc[:, g, h * D:(h + 1) * D], in_=wg[(h, g)][:])

        def units(b):
            return ((2 * b[0], b[1]), (2 * b[0] + 1, b[1]))

        def mm(b):
            for c, h in units(b):
                k = BATCHES.index(b) * 2 + c % 2
                acc = bank(UNIT_BANK[k], "pu", [P, 2, D], F32)
                pu[(c, h)] = acc
                for j in range(2):
                    cols = slice(j * P, (j + 1) * P)
                    for g in range(G):
                        nc.tensor.matmul_mx(out=acc[:, j, :], lhsT=xq[c][:, g, cols].bitcast(FP8X4), lhsT_scale=xsc[c][:, g, cols], rhs=wq[:, g, h * D:(h + 1) * D].bitcast(FP8X4), rhs_scale=wsc[:, g, h * D:(h + 1) * D], start=(g == 0), stop=(g == G - 1))

        def badd(b, i):
            c, h = units(b)[i]
            nc.vector.tensor_tensor(out=hh[c][:, :, h, :], in0=pu[(c, h)][:], in1=bias[:, h * D:(h + 1) * D].unsqueeze(1).to_broadcast([P, 2, D]), op=ALU.add)

        def square_tile(b, k, eng):
            c, h = units(b)[k // 2]
            tile_h = hh[c][:, k % 2, h, :]
            dump = junk[:, BATCHES.index(b), k, :]
            if eng == "S":
                nc.scalar.activation(out=dump, in_=tile_h, func=ACT.Square, accum_out=ss[b][:, k:k + 1])
            else:
                nc.vector.scalar_tensor_tensor(out=dump, in0=tile_h, scalar=1.0, in1=tile_h, op0=ALU.mult, op1=ALU.mult, accum_out=ss[b][:, k:k + 1])

        def square(b):
            for k in range(4):
                square_tile(b, k, "S")

        def root(b, lo=0, hi=4):
            nc.scalar.activation(out=rr[b][:, lo:hi], in_=ss[b][:, lo:hi], func=ACT.Abs_reciprocal_sqrt)

        def rmax(b, lo=0, hi=4):
            nc.vector.tensor_scalar_min(out=ri[b][:, lo:hi], in0=rr[b][:, lo:hi], scalar1=1e12)

        def scale(b, items, eng):
            for k in items:
                c, h = units(b)[k // 2]
                j = k % 2
                if eng == "S":
                    nc.scalar.activation(out=oo[c][:, j, h, :], in_=hh[c][:, j, h, :], func=ACT.Copy, scale=ri[b][:, k:k + 1])
                else:
                    nc.vector.tensor_scalar(out=oo[c][:, j, h, :], in0=hh[c][:, j, h, :], scalar1=ri[b][:, k:k + 1], scalar2=None, op0=ALU.mult)
                if eng == "V":
                    store(b, (k,))

        def store(b, items):
            for k in items:
                c, h = units(b)[k // 2]
                nc.sync.dma_start(out=outv[h, 2 * c + k % 2], in_=oo[c][:, k % 2, h, :])

        for g in range(G):
            for t in range(4):
                widen(0, g, t)
                widen(1, g, t)
                if (g, t) == (0, 0):
                    dummy(7)
                    dummy(7)
            if g == 0:
                xident(3, 0)
        wtrans(0, 0)
        wtrans(0, 1)
        wtrans(1, 0)
        wtrans(1, 1)
        inter(0, 0)
        inter(0, 1)
        inter(1, 0)
        inter(1, 1)
        xquant(0)
        xquant(1)
        xcopy(3, 0)
        wcopy(0, 0)
        wcopy(0, 1)
        bias_matmul()
        xident(3, 1)
        wtrans(2, 0)
        wtrans(2, 1)
        wquant(0, 0)
        wquant(0, 1)
        wcopy(1, 0)
        wcopy(1, 1)
        mm(BATCHES[0])
        bias_copy()
        inter(2, 0)
        inter(2, 1)
        wquant(1, 0)
        wquant(1, 1)
        mm(BATCHES[1])
        wcopy(2, 0)
        wcopy(2, 1)
        xcopy(3, 1)
        for i, b in enumerate(BATCHES[:-1]):
            prev = BATCHES[i - 1] if i > 0 else None
            prev2 = BATCHES[i - 2] if i > 1 else None
            badd(b, 0)
            badd(b, 1)
            if i == 0:
                xquant(2)
                wquant(2, 0)
                wquant(2, 1)
                mm(BATCHES[2])
            if i >= 2 and i + 2 < len(BATCHES):
                mm(BATCHES[i + 2])
            square(b)
            if prev:
                rmax(prev)
            if i == 1:
                xquant(3)
                mm(BATCHES[3])
            if prev2:
                scale(prev2, (1, 2), "V")
            if prev:
                scale(prev, (0,), "V")
                scale(prev, (3,), "S")
                store(prev, (3,))
            root(b)
        prev2, prev, last = BATCHES[-3], BATCHES[-2], BATCHES[-1]
        badd(last, 0)
        badd(last, 1)
        square_tile(last, 0, "S")
        square_tile(last, 1, "S")
        square_tile(last, 2, "S")
        rmax(prev)
        scale(prev2, (1, 2), "V")
        root(last, 0, 2)
        scale(prev, (0,), "V")
        scale(prev, (3,), "S")
        square_tile(last, 3, "V")
        root(last, 2, 4)
        scale(prev, (1,), "V")
        scale(prev, (2,), "V")
        store(prev, (3,))
        rmax(last, 0, 2)
        rmax(last, 2, 4)
        scale(last, (0,), "V")
        scale(last, (3,), "S")
        scale(last, (1, 2), "V")
        store(last, (3,))
